import numpy as np
import ml_dtypes


def mxq(x, axis, fmt="e4m3"):
    dtype, down = {"e4m3": (ml_dtypes.float8_e4m3fn, 7), "e5m2": (ml_dtypes.float8_e5m2, 14)}[fmt]
    v = np.moveaxis(np.asarray(x, np.float32).astype(ml_dtypes.bfloat16).astype(np.float64), axis, -1)
    blocks = v.reshape(v.shape[:-1] + (-1, 32))
    amax = np.abs(blocks).max(-1, keepdims=True)
    byte = np.maximum(np.where(amax > 0, np.frexp(amax)[1] - 1 + 127, 0) - down, 1)
    scale = np.exp2(byte - 127.0)
    codes = (blocks / scale).astype(np.float32).astype(dtype).astype(np.float64)
    return np.moveaxis((codes * scale).reshape(v.shape), -1, axis)


WIDE = False


def mx_kscale(k):
    if not WIDE:
        return np.ones(k)
    levels = np.array([10, -10, 5, -5, 0])
    if k % 512:
        return np.exp2(np.random.permutation(np.resize(levels, k // 32))).repeat(32)
    a = np.empty((k // 512, 16))
    for p in range(k // 512):
        a[p, :8] = np.random.permutation(np.resize(levels, 8))
        for g in range(8):
            far = levels[np.abs(levels - a[p, g]) >= 10]
            a[p, g + 8] = far[np.random.randint(len(far))]
    return np.exp2(a.ravel()).repeat(32)


BF16 = ml_dtypes.bfloat16


def bf(x):
    return np.asarray(x, np.float32).astype(BF16)


def f64(x):
    return np.asarray(x).astype(np.float64)


B, L, D, CH, S, R, NL = 1, 384, 1024, 2, 8, 128, 4
EPS = 1e-6


def rmsnorm(v, w):
    return v / np.sqrt(np.mean(v * v, axis=-1, keepdims=True) + EPS) * w


def setup_inputs():
    n = np.random.standard_normal
    t = mx_kscale(CH * D)
    return {"y": bf(n((B, L, CH * D)) * 0.9 * t),
            "x": bf(n((B, L, D))),
            "step_emb": bf(n(D) * 0.3),
            "out_proj_w": bf(n((D, CH * D)) / np.sqrt(CH * D) / t[None, :]),
            "mixer_norm_w": bf(1.0 + 0.1 * n(D)),
            "loop_norm_w": bf(1.0 + 0.1 * n(D))}


def reference(y, x, step_emb, out_proj_w, mixer_norm_w, loop_norm_w):
    h = f64(x) + f64(step_emb)
    out = rmsnorm(mxq(f64(y), 2, "e4m3") @ mxq(f64(out_proj_w), 1, "e4m3").T, f64(mixer_norm_w))
    return rmsnorm(h + out, f64(loop_norm_w))

@@ -1,0 +1,221 @@
+from contextlib import ExitStack
+
+import concourse.mybir as mybir
+from concourse.masks import make_identity
+
+F32 = mybir.dt.float32
+BF16 = mybir.dt.bfloat16
+I32 = mybir.dt.int32
+U32 = mybir.dt.uint32
+U8 = mybir.dt.uint8
+FP8X4 = mybir.dt.float8_e4m3fn_x4
+ACT = mybir.ActivationFunctionType
+ALU = mybir.AluOpType
+
+P = 128
+L, D, K = 384, 1024, 2048
+EPS = 1e-6
+PACK = 4
+PASSES = K // (P * PACK)
+BANK_PASSES = 2
+TILE_BANKS = PASSES // BANK_PASSES
+L_TILES = L // P
+CHUNK = 256
+CHUNK_TILES = CHUNK // P
+CHUNKS = D // CHUNK
+BANK = 512
+BANKS = D // BANK
+VECTOR_EVERY = 3
+
+FLOPS = 2 * L * D * K
+
+
+def tile_recursivemamba130m_pb_kernel(
+    tc, y, x, step_emb, out_proj_w, mixer_norm_w, loop_norm_w, out
+):
+    nc = tc.nc
+    y_rows = y.flatten_outer_dims()
+    x_rows = x.flatten_outer_dims()
+    out_rows = out.flatten_outer_dims()
+
+    with ExitStack() as ctx:
+        ctx.enter_context(tc.manual_schedule())
+        consts = ctx.enter_context(tc.tile_pool(name="consts", bufs=1))
+        raw = ctx.enter_context(tc.tile_pool(name="raw", bufs=1))
+        mx = ctx.enter_context(tc.tile_pool(name="mx", bufs=1))
+        stage = ctx.enter_context(tc.tile_pool(name="stage", bufs=2))
+        keep = ctx.enter_context(tc.tile_pool(name="keep", bufs=1))
+        scrap = ctx.enter_context(tc.tile_pool(name="scrap", bufs=2))
+        stats = ctx.enter_context(tc.tile_pool(name="stats", bufs=1))
+        tr_psum = ctx.enter_context(tc.psum_pool(name="tr_psum", bufs=4))
+        acc_psum = ctx.enter_context(tc.psum_pool(name="acc_psum", bufs=4))
+
+        vec_in = consts.tile([1, 3, D], BF16)
+        for i, vec in enumerate((mixer_norm_w, step_emb, loop_norm_w)):
+            nc.sync.dma_start(out=vec_in[:, i, :], in_=vec.unsqueeze(0))
+        w_raw = [raw.tile([P, CHUNK_TILES, K], BF16, name="w_raw%d" % c) for c in range(CHUNKS)]
+        for c in range(CHUNKS):
+            nc.sync.dma_start(
+                out=w_raw[c][:],
+                in_=out_proj_w[c * CHUNK : (c + 1) * CHUNK, :].rearrange("(i p) k -> p i k", p=P),
+            )
+        y_raw = [raw.tile([P, K], BF16, name="y_raw%d" % t) for t in range(L_TILES)]
+        for t in range(L_TILES):
+            nc.sync.dma_start(out=y_raw[t][:], in_=y_rows[t * P : (t + 1) * P, :])
+        x_raw = [raw.tile([P, D], BF16, name="x_raw%d" % t) for t in range(L_TILES)]
+        for t in range(L_TILES):
+            nc.sync.dma_start(out=x_raw[t][:], in_=x_rows[t * P : (t + 1) * P, :])
+
+        eps = consts.tile([P, 1], F32)
+        nc.vector.memset(eps[:], EPS)
+        warm = consts.tile([P, 1], F32)
+        nc.scalar.activation(out=warm[:], in_=eps[:], func=ACT.Abs_reciprocal_sqrt)
+        ident = consts.tile([P, P], F32)
+        make_identity(nc, ident[:])
+        ones = consts.tile([P, P], BF16)
+        nc.vector.memset(ones[:], 1.0)
+
+        vec_rows = consts.tile([P, 3, D], BF16)
+        nc.vector.memset(vec_rows[:].bitcast(I32), 0)
+        nc.vector.tensor_copy(out=vec_rows[0:1, :, :], in_=vec_in[:])
+        spread = consts.tile([P, 3, D], BF16)
+        for i in range(3):
+            bank = tr_psum.tile([P, D], BF16, name="bank")
+            for n in range(BANKS):
+                cols = slice(n * BANK, (n + 1) * BANK)
+                nc.tensor.matmul(
+                    out=bank[:, cols], lhsT=ones[:], rhs=vec_rows[:, i, cols], start=True, stop=True
+                )
+            nc.scalar.copy(out=spread[:, i, :], in_=bank[:])
+        mixer_gain = spread[:, 0, :]
+        step_row = spread[:, 1, :]
+        loop_gain = spread[:, 2, :]
+
+        def quantise_rows(row_tiles, staged, codes, scales, first_bank):
+            staged_words = staged[:].bitcast(F32)
+            for i, rows in enumerate(row_tiles):
+                row_words = rows.bitcast(F32)
+                for b in range(TILE_BANKS):
+                    bank = tr_psum.tile([P, BANK_PASSES, 2, P], F32, name="bank")
+                    for g in range(BANK_PASSES):
+                        for u in range(2):
+                            first = (b * BANK_PASSES + g) * 2 * P
+                            nc.tensor.transpose(
+                                bank[:, g, u, :],
+                                row_words[:, first + u : first + 2 * P : 2],
+                                ident[:],
+                            )
+                    passes = slice(b * BANK_PASSES, (b + 1) * BANK_PASSES)
+                    dst = staged_words[:, passes, i * P : (i + 1) * P, :]
+                    src = bank[:].rearrange("p g u r -> p g r u")
+                    if (first_bank + i * TILE_BANKS + b) % VECTOR_EVERY == 0:
+                        nc.vector.tensor_copy(out=dst, in_=src)
+                    else:
+                        nc.scalar.copy(out=dst, in_=src)
+            for g in range(PASSES):
+                nc.vector.quantize_mx(
+                    out=codes[:, g, :].bitcast(FP8X4),
+                    scales=scales[:, g, :],
+                    in_=staged[:, g, :, :].rearrange("p r t -> p (r t)"),
+                )
+
+        w_codes = mx.tile([P, PASSES, D], U32, align_bytes=64)
+        w_scales = mx.tile([P, PASSES, D], U8, align_bytes=64)
+        y_codes = mx.tile([P, PASSES, L], U32, align_bytes=64)
+        y_scales = mx.tile([P, PASSES, L], U8, align_bytes=64)
+
+        for c in range(CHUNKS):
+            w_staged = stage.tile([P, PASSES, CHUNK, PACK], BF16, align_bytes=64)
+            rows = slice(c * CHUNK, (c + 1) * CHUNK)
+            quantise_rows(
+                [w_raw[c][:, i, :] for i in range(CHUNK_TILES)],
+                w_staged, w_codes[:, :, rows], w_scales[:, :, rows], c * CHUNK_TILES * TILE_BANKS,
+            )
+        for t in range(L_TILES):
+            y_staged = stage.tile([P, PASSES, P, PACK], BF16, align_bytes=64)
+            rows = slice(t * P, (t + 1) * P)
+            quantise_rows(
+                [y_raw[t][:]], y_staged, y_codes[:, :, rows], y_scales[:, :, rows],
+                (D // P + t) * TILE_BANKS,
+            )
+
+        h = [keep.tile([P, D], F32, name="h%d" % t) for t in range(L_TILES)]
+        for t in range(L_TILES):
+            for c in range(CHUNKS):
+                cols = slice(c * CHUNK, (c + 1) * CHUNK)
+                nc.gpsimd.tensor_tensor(
+                    out=h[t][:, cols], in0=x_raw[t][:, cols], in1=step_row[:, cols], op=ALU.add
+                )
+
+        gained = [keep.tile([P, D], F32, name="gained%d" % t) for t in range(L_TILES)]
+        v = [keep.tile([P, D], F32, name="v%d" % t) for t in range(L_TILES)]
+        p_squares = [stats.tile([P, BANKS], F32, name="p_squares%d" % t) for t in range(L_TILES)]
+
+        def project(t):
+            folded = eps
+            for n in range(BANKS):
+                cols = slice(n * BANK, (n + 1) * BANK)
+                acc = acc_psum.tile([P, BANK], F32)
+                for g in range(PASSES):
+                    nc.tensor.matmul_mx(
+                        out=acc[:],
+                        lhsT=y_codes[:, g, t * P : (t + 1) * P].bitcast(FP8X4),
+                        lhsT_scale=y_scales[:, g, t * P : (t + 1) * P],
+                        rhs=w_codes[:, g, cols].bitcast(FP8X4),
+                        rhs_scale=w_scales[:, g, cols],
+                        start=(g == 0),
+                        stop=(g == PASSES - 1),
+                    )
+                squares = scrap.tile([P, BANK], BF16, name="squares")
+                nc.scalar.activation(
+                    out=squares[:], in_=acc[:], func=ACT.Square,
+                    accum_out=p_squares[t][:, n : n + 1],
+                )
+                nc.vector.tensor_tensor(
+                    out=gained[t][:, cols], in0=acc[:], in1=mixer_gain[:, cols], op=ALU.mult
+                )
+                if n + 1 < BANKS:
+                    share = stats.tile([P, 1], F32, name="share%d_%d" % (t, n))
+                    nc.scalar.activation(
+                        out=share[:], in_=p_squares[t][:, n : n + 1], func=ACT.Identity,
+                        scale=1.0 / D, bias=folded[:],
+                    )
+                    folded = share
+            return folded
+
+        def inverse_rms(sum_of_squares, rest, name):
+            inv = stats.tile([P, 1], F32, name="inv_" + name)
+            nc.scalar.activation(
+                out=inv[:], in_=sum_of_squares, func=ACT.Abs_reciprocal_sqrt,
+                scale=1.0 / D, bias=rest[:],
+            )
+            return inv
+
+        def first_norm(t, folded):
+            inv_p = inverse_rms(p_squares[t][:, BANKS - 1 : BANKS], folded, "p%d" % t)
+            nc.vector.scalar_tensor_tensor(
+                out=v[t][:], in0=gained[t][:], scalar=inv_p[:], in1=h[t][:],
+                op0=ALU.mult, op1=ALU.add,
+            )
+
+        def second_norm(t):
+            v_squares = scrap.tile([P, D], BF16, name="v_squares")
+            v_square_sum = stats.tile([P, 1], F32, name="v_square_sum%d" % t)
+            nc.scalar.activation(
+                out=v_squares[:], in_=v[t][:], func=ACT.Square, accum_out=v_square_sum[:]
+            )
+            inv_v = inverse_rms(v_square_sum[:], eps, "v%d" % t)
+            result = scrap.tile([P, D], F32, name="result")
+            for n in range(BANKS):
+                cols = slice(n * BANK, (n + 1) * BANK)
+                nc.vector.scalar_tensor_tensor(
+                    out=result[:, cols], in0=v[t][:, cols], scalar=inv_v[:], in1=loop_gain[:, cols],
+                    op0=ALU.mult, op1=ALU.mult,
+                )
+                nc.sync.dma_start(out=out_rows[t * P : (t + 1) * P, cols], in_=result[:, cols])
+
+        first_norm(0, project(0))
+        for t in range(1, L_TILES):
+            first_norm(t, project(t))
+            second_norm(t - 1)
+        second_norm(L_TILES - 1)

@@ -17,15 +17,15 @@ L, D, K = 384, 1024, 2048
 EPS = 1e-6
 PACK = 4
 PASSES = K // (P * PACK)
-BANK_PASSES = 2
-TILE_BANKS = PASSES // BANK_PASSES
+PASS_WORDS = 2 * P
 L_TILES = L // P
 CHUNK = 256
 CHUNK_TILES = CHUNK // P
 CHUNKS = D // CHUNK
+HALF = K // 2
+HALF_PASSES = PASSES // 2
 BANK = 512
 BANKS = D // BANK
-VECTOR_EVERY = 3
 
 FLOPS = 2 * L * D * K
 
@@ -43,28 +43,52 @@ def tile_recursivemamba130m_pb_kernel(
         consts = ctx.enter_context(tc.tile_pool(name="consts", bufs=1))
         raw = ctx.enter_context(tc.tile_pool(name="raw", bufs=1))
         mx = ctx.enter_context(tc.tile_pool(name="mx", bufs=1))
-        stage = ctx.enter_context(tc.tile_pool(name="stage", bufs=2))
+        stage = ctx.enter_context(tc.tile_pool(name="stage", bufs=8))
         keep = ctx.enter_context(tc.tile_pool(name="keep", bufs=1))
         scrap = ctx.enter_context(tc.tile_pool(name="scrap", bufs=2))
         stats = ctx.enter_context(tc.tile_pool(name="stats", bufs=1))
-        tr_psum = ctx.enter_context(tc.psum_pool(name="tr_psum", bufs=4))
-        acc_psum = ctx.enter_context(tc.psum_pool(name="acc_psum", bufs=4))
+        tr_psum = ctx.enter_context(tc.psum_pool(name="tr_psum", bufs=3))
+        acc_psum = ctx.enter_context(tc.psum_pool(name="acc_psum", bufs=3))
+        vec_psum = ctx.enter_context(tc.psum_pool(name="vec_psum", bufs=1))
 
         vec_in = consts.tile([1, 3, D], BF16)
+        y_raw = [raw.tile([P, K], BF16, name="y_raw%d" % t) for t in range(L_TILES)]
+        w_raw = [
+            [raw.tile([P, CHUNK_TILES, HALF], BF16, name="w_raw%d_%d" % (c, s)) for s in range(2)]
+            for c in range(CHUNKS)
+        ]
+        x_raw = [raw.tile([P, D], BF16, name="x_raw%d" % t) for t in range(L_TILES)]
+
+        def load_y(t, pieces):
+            for cols in pieces:
+                nc.sync.dma_start(out=y_raw[t][:, cols], in_=y_rows[t * P : (t + 1) * P, cols])
+
+        def load_x(t):
+            nc.sync.dma_start(out=x_raw[t][:], in_=x_rows[t * P : (t + 1) * P, :])
+
+        def load_w(c):
+            for s in range(2):
+                nc.sync.dma_start(
+                    out=w_raw[c][s][:],
+                    in_=out_proj_w[c * CHUNK : (c + 1) * CHUNK, s * HALF : (s + 1) * HALF].rearrange(
+                        "(i p) k -> p i k", p=P
+                    ),
+                )
+
+        whole = [slice(0, K)]
+        halves = [slice(0, HALF), slice(HALF, K)]
+        load_y(0, halves)
         for i, vec in enumerate((mixer_norm_w, step_emb, loop_norm_w)):
             nc.sync.dma_start(out=vec_in[:, i, :], in_=vec.unsqueeze(0))
-        w_raw = [raw.tile([P, CHUNK_TILES, K], BF16, name="w_raw%d" % c) for c in range(CHUNKS)]
-        for c in range(CHUNKS):
-            nc.sync.dma_start(
-                out=w_raw[c][:],
-                in_=out_proj_w[c * CHUNK : (c + 1) * CHUNK, :].rearrange("(i p) k -> p i k", p=P),
-            )
-        y_raw = [raw.tile([P, K], BF16, name="y_raw%d" % t) for t in range(L_TILES)]
-        for t in range(L_TILES):
-            nc.sync.dma_start(out=y_raw[t][:], in_=y_rows[t * P : (t + 1) * P, :])
-        x_raw = [raw.tile([P, D], BF16, name="x_raw%d" % t) for t in range(L_TILES)]
-        for t in range(L_TILES):
-            nc.sync.dma_start(out=x_raw[t][:], in_=x_rows[t * P : (t + 1) * P, :])
+        load_w(0)
+        load_x(0)
+        load_x(1)
+        load_w(1)
+        load_x(2)
+        load_w(2)
+        load_w(3)
+        load_y(1, whole)
+        load_y(2, whole)
 
         eps = consts.tile([P, 1], F32)
         nc.vector.memset(eps[:], EPS)
@@ -78,144 +102,233 @@ def tile_recursivemamba130m_pb_kernel(
         vec_rows = consts.tile([P, 3, D], BF16)
         nc.vector.memset(vec_rows[:].bitcast(I32), 0)
         nc.vector.tensor_copy(out=vec_rows[0:1, :, :], in_=vec_in[:])
-        spread = consts.tile([P, 3, D], BF16)
-        for i in range(3):
-            bank = tr_psum.tile([P, D], BF16, name="bank")
+        mixer_gain = consts.tile([P, D], BF16)
+        step_row = vec_psum.tile([P, D], BF16)
+        loop_gain = vec_psum.tile([P, D], BF16)
+
+        def spread(i, bank):
             for n in range(BANKS):
                 cols = slice(n * BANK, (n + 1) * BANK)
                 nc.tensor.matmul(
                     out=bank[:, cols], lhsT=ones[:], rhs=vec_rows[:, i, cols], start=True, stop=True
                 )
-            nc.scalar.copy(out=spread[:, i, :], in_=bank[:])
-        mixer_gain = spread[:, 0, :]
-        step_row = spread[:, 1, :]
-        loop_gain = spread[:, 2, :]
-
-        def quantise_rows(row_tiles, staged, codes, scales, first_bank):
-            staged_words = staged[:].bitcast(F32)
-            for i, rows in enumerate(row_tiles):
-                row_words = rows.bitcast(F32)
-                for b in range(TILE_BANKS):
-                    bank = tr_psum.tile([P, BANK_PASSES, 2, P], F32, name="bank")
-                    for g in range(BANK_PASSES):
-                        for u in range(2):
-                            first = (b * BANK_PASSES + g) * 2 * P
-                            nc.tensor.transpose(
-                                bank[:, g, u, :],
-                                row_words[:, first + u : first + 2 * P : 2],
-                                ident[:],
-                            )
-                    passes = slice(b * BANK_PASSES, (b + 1) * BANK_PASSES)
-                    dst = staged_words[:, passes, i * P : (i + 1) * P, :]
-                    src = bank[:].rearrange("p g u r -> p g r u")
-                    if (first_bank + i * TILE_BANKS + b) % VECTOR_EVERY == 0:
-                        nc.vector.tensor_copy(out=dst, in_=src)
-                    else:
-                        nc.scalar.copy(out=dst, in_=src)
-            for g in range(PASSES):
-                nc.vector.quantize_mx(
-                    out=codes[:, g, :].bitcast(FP8X4),
-                    scales=scales[:, g, :],
-                    in_=staged[:, g, :, :].rearrange("p r t -> p (r t)"),
-                )
 
         w_codes = mx.tile([P, PASSES, D], U32, align_bytes=64)
         w_scales = mx.tile([P, PASSES, D], U8, align_bytes=64)
-        y_codes = mx.tile([P, PASSES, L], U32, align_bytes=64)
-        y_scales = mx.tile([P, PASSES, L], U8, align_bytes=64)
+        y_codes = mx.tile([P, L_TILES, PASSES, P], U32, align_bytes=64)
+        y_scales = mx.tile([P, L_TILES, PASSES, P], U8, align_bytes=64)
 
-        for c in range(CHUNKS):
-            w_staged = stage.tile([P, PASSES, CHUNK, PACK], BF16, align_bytes=64)
-            rows = slice(c * CHUNK, (c + 1) * CHUNK)
-            quantise_rows(
-                [w_raw[c][:, i, :] for i in range(CHUNK_TILES)],
-                w_staged, w_codes[:, :, rows], w_scales[:, :, rows], c * CHUNK_TILES * TILE_BANKS,
+        def w_unit(c, g):
+            s, first = g // HALF_PASSES, (g % HALF_PASSES) * PASS_WORDS
+            cols = slice(c * CHUNK, (c + 1) * CHUNK)
+            blocks = [(w_raw[c][s][:, i, :].bitcast(F32), first) for i in range(CHUNK_TILES)]
+            return blocks, w_codes[:, g, cols], w_scales[:, g, cols]
+
+        def y_unit(t, s):
+            passes = slice(s * HALF_PASSES, (s + 1) * HALF_PASSES)
+            blocks = [
+                (y_raw[t][:].bitcast(F32), g * PASS_WORDS)
+                for g in range(s * HALF_PASSES, (s + 1) * HALF_PASSES)
+            ]
+            return (
+                blocks,
+                y_codes[:, t, passes, :].rearrange("p g r -> p (g r)"),
+                y_scales[:, t, passes, :].rearrange("p g r -> p (g r)"),
             )
-        for t in range(L_TILES):
-            y_staged = stage.tile([P, PASSES, P, PACK], BF16, align_bytes=64)
-            rows = slice(t * P, (t + 1) * P)
-            quantise_rows(
-                [y_raw[t][:]], y_staged, y_codes[:, :, rows], y_scales[:, :, rows],
-                (D // P + t) * TILE_BANKS,
+
+        def transpose(unit):
+            bank = tr_psum.tile([P, 2, 2, P], F32, name="bank")
+            for i, (words, first) in enumerate(unit[0]):
+                for u in range(2):
+                    nc.tensor.transpose(
+                        bank[:, i, u, :], words[:, first + u : first + PASS_WORDS : 2], ident[:]
+                    )
+            return bank
+
+        def empty(bank, copy):
+            staged = stage.tile([P, 2, P, PACK], BF16, align_bytes=64, name="staged")
+            copy(out=staged[:].bitcast(F32), in_=bank[:].rearrange("p i u r -> p i r u"))
+            return staged
+
+        def quantise(unit, staged):
+            nc.vector.quantize_mx(
+                out=unit[1].bitcast(FP8X4),
+                scales=unit[2],
+                in_=staged[:].rearrange("p i r t -> p (i r t)"),
             )
 
         h = [keep.tile([P, D], F32, name="h%d" % t) for t in range(L_TILES)]
-        for t in range(L_TILES):
-            for c in range(CHUNKS):
-                cols = slice(c * CHUNK, (c + 1) * CHUNK)
-                nc.gpsimd.tensor_tensor(
-                    out=h[t][:, cols], in0=x_raw[t][:, cols], in1=step_row[:, cols], op=ALU.add
-                )
-
         gained = [keep.tile([P, D], F32, name="gained%d" % t) for t in range(L_TILES)]
         v = [keep.tile([P, D], F32, name="v%d" % t) for t in range(L_TILES)]
+        result = [keep.tile([P, D], F32, name="result%d" % t) for t in range(L_TILES)]
         p_squares = [stats.tile([P, BANKS], F32, name="p_squares%d" % t) for t in range(L_TILES)]
+        v_squares = [stats.tile([P, BANKS], F32, name="v_squares%d" % t) for t in range(L_TILES)]
 
-        def project(t):
-            folded = eps
-            for n in range(BANKS):
-                cols = slice(n * BANK, (n + 1) * BANK)
-                acc = acc_psum.tile([P, BANK], F32)
-                for g in range(PASSES):
-                    nc.tensor.matmul_mx(
-                        out=acc[:],
-                        lhsT=y_codes[:, g, t * P : (t + 1) * P].bitcast(FP8X4),
-                        lhsT_scale=y_scales[:, g, t * P : (t + 1) * P],
-                        rhs=w_codes[:, g, cols].bitcast(FP8X4),
-                        rhs_scale=w_scales[:, g, cols],
-                        start=(g == 0),
-                        stop=(g == PASSES - 1),
-                    )
-                squares = scrap.tile([P, BANK], BF16, name="squares")
-                nc.scalar.activation(
-                    out=squares[:], in_=acc[:], func=ACT.Square,
-                    accum_out=p_squares[t][:, n : n + 1],
-                )
-                nc.vector.tensor_tensor(
-                    out=gained[t][:, cols], in0=acc[:], in1=mixer_gain[:, cols], op=ALU.mult
-                )
-                if n + 1 < BANKS:
-                    share = stats.tile([P, 1], F32, name="share%d_%d" % (t, n))
-                    nc.scalar.activation(
-                        out=share[:], in_=p_squares[t][:, n : n + 1], func=ACT.Identity,
-                        scale=1.0 / D, bias=folded[:],
-                    )
-                    folded = share
-            return folded
+        def columns(n):
+            return slice(n * BANK, (n + 1) * BANK)
 
-        def inverse_rms(sum_of_squares, rest, name):
+        def residual(t, n):
+            nc.vector.tensor_tensor(
+                out=h[t][:, columns(n)], in0=x_raw[t][:, columns(n)], in1=step_row[:, columns(n)],
+                op=ALU.add,
+            )
+
+        def product(t, n):
+            acc = acc_psum.tile([P, BANK], F32, name="acc")
+            for g in range(PASSES):
+                nc.tensor.matmul_mx(
+                    out=acc[:],
+                    lhsT=y_codes[:, t, g, :].bitcast(FP8X4),
+                    lhsT_scale=y_scales[:, t, g, :],
+                    rhs=w_codes[:, g, columns(n)].bitcast(FP8X4),
+                    rhs_scale=w_scales[:, g, columns(n)],
+                    start=(g == 0),
+                    stop=(g == PASSES - 1),
+                )
+            return acc
+
+        def mean_share(squares, n, rest, name):
+            share = stats.tile([P, 1], F32, name="share_" + name)
+            nc.scalar.activation(
+                out=share[:], in_=squares[:, n : n + 1], func=ACT.Identity,
+                scale=1.0 / D, bias=rest[:],
+            )
+            return share
+
+        def inverse_rms(squares, rest, name):
             inv = stats.tile([P, 1], F32, name="inv_" + name)
             nc.scalar.activation(
-                out=inv[:], in_=sum_of_squares, func=ACT.Abs_reciprocal_sqrt,
+                out=inv[:], in_=squares[:, BANKS - 1 : BANKS], func=ACT.Abs_reciprocal_sqrt,
                 scale=1.0 / D, bias=rest[:],
             )
             return inv
 
-        def first_norm(t, folded):
-            inv_p = inverse_rms(p_squares[t][:, BANKS - 1 : BANKS], folded, "p%d" % t)
-            nc.vector.scalar_tensor_tensor(
-                out=v[t][:], in0=gained[t][:], scalar=inv_p[:], in1=h[t][:],
-                op0=ALU.mult, op1=ALU.add,
+        def square_sum(src, sums, n):
+            squares = scrap.tile([P, BANK], BF16, name="squares")
+            nc.scalar.activation(
+                out=squares[:], in_=src, func=ACT.Square, accum_out=sums[:, n : n + 1]
             )
+
+        def square_p(t, n, acc):
+            square_sum(acc[:], p_squares[t], n)
+
+        def gain(t, n, acc):
+            nc.vector.tensor_tensor(
+                out=gained[t][:, columns(n)], in0=acc[:], in1=mixer_gain[:, columns(n)], op=ALU.mult
+            )
+
+        def first_scale(t):
+            return inverse_rms(
+                p_squares[t], mean_share(p_squares[t], 0, eps, "p%d" % t), "p%d" % t
+            )
+
+        def first_norm(t, inv_p):
+            for n in range(BANKS):
+                nc.vector.scalar_tensor_tensor(
+                    out=v[t][:, columns(n)], in0=gained[t][:, columns(n)], scalar=inv_p[:],
+                    in1=h[t][:, columns(n)], op0=ALU.mult, op1=ALU.add,
+                )
+
+        def sum_v(t):
+            for n in range(BANKS):
+                square_sum(v[t][:, columns(n)], v_squares[t], n)
 
         def second_norm(t):
-            v_squares = scrap.tile([P, D], BF16, name="v_squares")
-            v_square_sum = stats.tile([P, 1], F32, name="v_square_sum%d" % t)
-            nc.scalar.activation(
-                out=v_squares[:], in_=v[t][:], func=ACT.Square, accum_out=v_square_sum[:]
+            inv_v = inverse_rms(
+                v_squares[t], mean_share(v_squares[t], 0, eps, "v%d" % t), "v%d" % t
             )
-            inv_v = inverse_rms(v_square_sum[:], eps, "v%d" % t)
-            result = scrap.tile([P, D], F32, name="result")
             for n in range(BANKS):
-                cols = slice(n * BANK, (n + 1) * BANK)
                 nc.vector.scalar_tensor_tensor(
-                    out=result[:, cols], in0=v[t][:, cols], scalar=inv_v[:], in1=loop_gain[:, cols],
-                    op0=ALU.mult, op1=ALU.mult,
+                    out=result[t][:, columns(n)], in0=v[t][:, columns(n)], scalar=inv_v[:],
+                    in1=loop_gain[:, columns(n)], op0=ALU.mult, op1=ALU.mult,
                 )
-                nc.sync.dma_start(out=out_rows[t * P : (t + 1) * P, cols], in_=result[:, cols])
+                nc.sync.dma_start(
+                    out=out_rows[t * P : (t + 1) * P, columns(n)], in_=result[t][:, columns(n)]
+                )
 
-        first_norm(0, project(0))
-        for t in range(1, L_TILES):
-            first_norm(t, project(t))
-            second_norm(t - 1)
-        second_norm(L_TILES - 1)
+        pending = []
+
+        def convert(unit, copy):
+            bank = transpose(unit)
+            if pending:
+                quantise(*pending.pop())
+            pending.append((unit, empty(bank, copy)))
+
+        def flush():
+            quantise(*pending.pop())
+
+        scopy, vcopy = nc.scalar.copy, nc.vector.tensor_copy
+
+        def convert_w(c, copies):
+            for g in range(PASSES):
+                convert(w_unit(c, g), copies[g % len(copies)])
+
+        def convert_y(t, copies):
+            for s in range(2):
+                convert(y_unit(t, s), copies[s % len(copies)])
+
+        def mixer():
+            bank = tr_psum.tile([P, D], BF16, name="bank")
+            spread(0, bank)
+            nc.vector.tensor_copy(out=mixer_gain[:], in_=bank[:])
+
+        h_pieces = [(t, n) for t in range(L_TILES) for n in range(BANKS)]
+
+        def residual_piece():
+            if h_pieces:
+                residual(*h_pieces.pop(0))
+
+        convert_y(0, [scopy])
+        mixer()
+        spread(1, step_row)
+        spread(2, loop_gain)
+        convert_w(0, [scopy])
+        for g in range(PASSES):
+            convert(w_unit(1, g), scopy)
+            if g % 2:
+                residual_piece()
+        for g in range(PASSES):
+            convert(w_unit(2, g), scopy)
+            if g % 2:
+                residual_piece()
+        acc = product(0, 0)
+        for g in range(PASSES):
+            convert(w_unit(3, g), scopy)
+            if g == 0:
+                square_p(0, 0, acc)
+            if g == 1:
+                gain(0, 0, acc)
+            if g % 2:
+                residual_piece()
+        convert(y_unit(1, 0), scopy)
+        convert(y_unit(1, 1), scopy)
+        acc01 = product(0, 1)
+        square_p(0, 1, acc01)
+        inv0 = first_scale(0)
+        convert(y_unit(2, 0), scopy)
+        gain(0, 1, acc01)
+        convert(y_unit(2, 1), scopy)
+        acc10 = product(1, 0)
+        first_norm(0, inv0)
+        flush()
+        square_p(1, 0, acc10)
+        sum_v(0)
+        gain(1, 0, acc10)
+        acc11 = product(1, 1)
+        second_norm(0)
+        square_p(1, 1, acc11)
+        inv1 = first_scale(1)
+        gain(1, 1, acc11)
+        acc20 = product(2, 0)
+        first_norm(1, inv1)
+        square_p(2, 0, acc20)
+        gain(2, 0, acc20)
+        acc21 = product(2, 1)
+        square_p(2, 1, acc21)
+        inv2 = first_scale(2)
+        sum_v(1)
+        gain(2, 1, acc21)
+        first_norm(2, inv2)
+        second_norm(1)
+        sum_v(2)
+        second_norm(2)

@@ -106,12 +106,24 @@ def tile_recursivemamba130m_pb_kernel(
         step_row = vec_psum.tile([P, D], BF16)
         loop_gain = vec_psum.tile([P, D], BF16)
 
-        def spread(i, bank):
-            for n in range(BANKS):
-                cols = slice(n * BANK, (n + 1) * BANK)
-                nc.tensor.matmul(
-                    out=bank[:, cols], lhsT=ones[:], rhs=vec_rows[:, i, cols], start=True, stop=True
-                )
+        def columns(n):
+            return slice(n * BANK, (n + 1) * BANK)
+
+        def spread(i, n, out):
+            nc.tensor.matmul(
+                out=out, lhsT=ones[:], rhs=vec_rows[:, i, columns(n)], start=True, stop=True
+            )
+
+        def spread_mixer(n):
+            bank = tr_psum.tile([P, BANK], BF16, name="bank")
+            spread(0, n, bank[:])
+            nc.vector.tensor_copy(out=mixer_gain[:, columns(n)], in_=bank[:])
+
+        def spread_step(n):
+            spread(1, n, step_row[:, columns(n)])
+
+        def spread_loop(n):
+            spread(2, n, loop_gain[:, columns(n)])
 
         w_codes = mx.tile([P, PASSES, D], U32, align_bytes=64)
         w_scales = mx.tile([P, PASSES, D], U8, align_bytes=64)
@@ -163,9 +175,6 @@ def tile_recursivemamba130m_pb_kernel(
         result = [keep.tile([P, D], F32, name="result%d" % t) for t in range(L_TILES)]
         p_squares = [stats.tile([P, BANKS], F32, name="p_squares%d" % t) for t in range(L_TILES)]
         v_squares = [stats.tile([P, BANKS], F32, name="v_squares%d" % t) for t in range(L_TILES)]
-
-        def columns(n):
-            return slice(n * BANK, (n + 1) * BANK)
 
         def residual(t, n):
             nc.vector.tensor_tensor(
@@ -267,50 +276,32 @@ def tile_recursivemamba130m_pb_kernel(
             for s in range(2):
                 convert(y_unit(t, s), copies[s % len(copies)])
 
-        def mixer():
-            bank = tr_psum.tile([P, D], BF16, name="bank")
-            spread(0, bank)
-            nc.vector.tensor_copy(out=mixer_gain[:], in_=bank[:])
-
         h_pieces = [(t, n) for t in range(L_TILES) for n in range(BANKS)]
-
-        def residual_piece():
-            if h_pieces:
-                residual(*h_pieces.pop(0))
-
+        units = [w_unit(c, g) for c in range(1, CHUNKS) for g in range(PASSES)]
+        units += [y_unit(t, s) for t in range(1, L_TILES) for s in range(2)]
         convert_y(0, [scopy])
-        mixer()
-        spread(1, step_row)
-        spread(2, loop_gain)
-        convert_w(0, [scopy])
         for g in range(PASSES):
-            convert(w_unit(1, g), scopy)
-            if g % 2:
-                residual_piece()
-        for g in range(PASSES):
-            convert(w_unit(2, g), scopy)
-            if g % 2:
-                residual_piece()
-        acc = product(0, 0)
-        for g in range(PASSES):
-            convert(w_unit(3, g), scopy)
-            if g == 0:
-                square_p(0, 0, acc)
-            if g == 1:
-                gain(0, 0, acc)
-            if g % 2:
-                residual_piece()
-        convert(y_unit(1, 0), scopy)
-        convert(y_unit(1, 1), scopy)
+            convert(w_unit(0, g), scopy)
+        for n in range(BANKS):
+            spread_step(n)
+        for n in range(BANKS):
+            spread_mixer(n)
+        for n in range(BANKS):
+            spread_loop(n)
+        for i, unit in enumerate(units):
+            convert(unit, scopy)
+            if i % 2 == 1 and h_pieces:
+                residual(*h_pieces.pop(0))
+        flush()
+        acc00 = product(0, 0)
+        square_p(0, 0, acc00)
+        gain(0, 0, acc00)
         acc01 = product(0, 1)
         square_p(0, 1, acc01)
         inv0 = first_scale(0)
-        convert(y_unit(2, 0), scopy)
         gain(0, 1, acc01)
-        convert(y_unit(2, 1), scopy)
         acc10 = product(1, 0)
         first_norm(0, inv0)
-        flush()
         square_p(1, 0, acc10)
         sum_v(0)
         gain(1, 0, acc10)

@@ -5,7 +5,6 @@ from concourse.masks import make_identity
 
 F32 = mybir.dt.float32
 BF16 = mybir.dt.bfloat16
-I32 = mybir.dt.int32
 U32 = mybir.dt.uint32
 U8 = mybir.dt.uint8
 FP8X4 = mybir.dt.float8_e4m3fn_x4
@@ -26,6 +25,9 @@ HALF = K // 2
 HALF_PASSES = PASSES // 2
 BANK = 512
 BANKS = D // BANK
+VEC_WORDS = D // 2 // P
+PIECE = 256
+PIECES = D // PIECE
 
 FLOPS = 2 * L * D * K
 
@@ -47,11 +49,10 @@ def tile_recursivemamba130m_pb_kernel(
         keep = ctx.enter_context(tc.tile_pool(name="keep", bufs=1))
         scrap = ctx.enter_context(tc.tile_pool(name="scrap", bufs=2))
         stats = ctx.enter_context(tc.tile_pool(name="stats", bufs=1))
-        tr_psum = ctx.enter_context(tc.psum_pool(name="tr_psum", bufs=3))
-        acc_psum = ctx.enter_context(tc.psum_pool(name="acc_psum", bufs=3))
-        vec_psum = ctx.enter_context(tc.psum_pool(name="vec_psum", bufs=1))
+        tr_psum = ctx.enter_context(tc.psum_pool(name="tr_psum", bufs=4))
+        acc_psum = ctx.enter_context(tc.psum_pool(name="acc_psum", bufs=4))
 
-        vec_in = consts.tile([1, 3, D], BF16)
+        vec_in = [consts.tile([P, D // P], BF16, name="vec_in%d" % i) for i in range(3)]
         y_raw = [raw.tile([P, K], BF16, name="y_raw%d" % t) for t in range(L_TILES)]
         w_raw = [
             [raw.tile([P, CHUNK_TILES, HALF], BF16, name="w_raw%d_%d" % (c, s)) for s in range(2)]
@@ -77,18 +78,15 @@ def tile_recursivemamba130m_pb_kernel(
 
         whole = [slice(0, K)]
         halves = [slice(0, HALF), slice(HALF, K)]
-        load_y(0, halves)
         for i, vec in enumerate((mixer_norm_w, step_emb, loop_norm_w)):
-            nc.sync.dma_start(out=vec_in[:, i, :], in_=vec.unsqueeze(0))
-        load_w(0)
-        load_x(0)
-        load_x(1)
-        load_w(1)
-        load_x(2)
-        load_w(2)
-        load_w(3)
-        load_y(1, whole)
-        load_y(2, whole)
+            nc.sync.dma_start(out=vec_in[i][:], in_=vec.rearrange("(p j) -> p j", p=P))
+        load_y(0, halves)
+        for c in range(CHUNKS):
+            load_w(c)
+        for t in range(1, L_TILES):
+            load_y(t, whole)
+        for t in range(L_TILES):
+            load_x(t)
 
         eps = consts.tile([P, 1], F32)
         nc.vector.memset(eps[:], EPS)
@@ -96,34 +94,22 @@ def tile_recursivemamba130m_pb_kernel(
         nc.scalar.activation(out=warm[:], in_=eps[:], func=ACT.Abs_reciprocal_sqrt)
         ident = consts.tile([P, P], F32)
         make_identity(nc, ident[:])
-        ones = consts.tile([P, P], BF16)
-        nc.vector.memset(ones[:], 1.0)
-
-        vec_rows = consts.tile([P, 3, D], BF16)
-        nc.vector.memset(vec_rows[:].bitcast(I32), 0)
-        nc.vector.tensor_copy(out=vec_rows[0:1, :, :], in_=vec_in[:])
-        mixer_gain = consts.tile([P, D], BF16)
-        step_row = vec_psum.tile([P, D], BF16)
-        loop_gain = vec_psum.tile([P, D], BF16)
+        def spread(i, copy):
+            words = vec_in[i][:].bitcast(F32)
+            bank = tr_psum.tile([P, VEC_WORDS, P], F32, name="bank")
+            for j in range(VEC_WORDS):
+                nc.tensor.transpose(
+                    bank[:, j, :], words[:, j : j + 1].to_broadcast([P, P]), ident[:]
+                )
+            row = consts.tile([P, D], BF16, name="row%d" % i)
+            copy(
+                out=row[:].bitcast(F32).rearrange("p (w j) -> p w j", j=VEC_WORDS),
+                in_=bank[:].rearrange("p j w -> p w j"),
+            )
+            return row
 
         def columns(n):
             return slice(n * BANK, (n + 1) * BANK)
-
-        def spread(i, n, out):
-            nc.tensor.matmul(
-                out=out, lhsT=ones[:], rhs=vec_rows[:, i, columns(n)], start=True, stop=True
-            )
-
-        def spread_mixer(n):
-            bank = tr_psum.tile([P, BANK], BF16, name="bank")
-            spread(0, n, bank[:])
-            nc.vector.tensor_copy(out=mixer_gain[:, columns(n)], in_=bank[:])
-
-        def spread_step(n):
-            spread(1, n, step_row[:, columns(n)])
-
-        def spread_loop(n):
-            spread(2, n, loop_gain[:, columns(n)])
 
         w_codes = mx.tile([P, PASSES, D], U32, align_bytes=64)
         w_scales = mx.tile([P, PASSES, D], U8, align_bytes=64)
@@ -176,11 +162,12 @@ def tile_recursivemamba130m_pb_kernel(
         p_squares = [stats.tile([P, BANKS], F32, name="p_squares%d" % t) for t in range(L_TILES)]
         v_squares = [stats.tile([P, BANKS], F32, name="v_squares%d" % t) for t in range(L_TILES)]
 
-        def residual(t, n):
-            nc.vector.tensor_tensor(
-                out=h[t][:, columns(n)], in0=x_raw[t][:, columns(n)], in1=step_row[:, columns(n)],
-                op=ALU.add,
-            )
+        def residual(t):
+            for q in range(PIECES):
+                cols = slice(q * PIECE, (q + 1) * PIECE)
+                nc.gpsimd.tensor_tensor(
+                    out=h[t][:, cols], in0=x_raw[t][:, cols], in1=step_row[:, cols], op=ALU.add
+                )
 
         def product(t, n):
             acc = acc_psum.tile([P, BANK], F32, name="acc")
@@ -196,19 +183,15 @@ def tile_recursivemamba130m_pb_kernel(
                 )
             return acc
 
-        def mean_share(squares, n, rest, name):
+        def inverse_rms(squares, name):
             share = stats.tile([P, 1], F32, name="share_" + name)
             nc.scalar.activation(
-                out=share[:], in_=squares[:, n : n + 1], func=ACT.Identity,
-                scale=1.0 / D, bias=rest[:],
+                out=share[:], in_=squares[:, 0:1], func=ACT.Identity, scale=1.0 / D, bias=eps[:]
             )
-            return share
-
-        def inverse_rms(squares, rest, name):
             inv = stats.tile([P, 1], F32, name="inv_" + name)
             nc.scalar.activation(
-                out=inv[:], in_=squares[:, BANKS - 1 : BANKS], func=ACT.Abs_reciprocal_sqrt,
-                scale=1.0 / D, bias=rest[:],
+                out=inv[:], in_=squares[:, 1:2], func=ACT.Abs_reciprocal_sqrt,
+                scale=1.0 / D, bias=share[:],
             )
             return inv
 
@@ -223,13 +206,11 @@ def tile_recursivemamba130m_pb_kernel(
 
         def gain(t, n, acc):
             nc.vector.tensor_tensor(
-                out=gained[t][:, columns(n)], in0=acc[:], in1=mixer_gain[:, columns(n)], op=ALU.mult
+                out=gained[t][:, columns(n)], in0=acc[:], in1=mixer_row[:, columns(n)], op=ALU.mult
             )
 
         def first_scale(t):
-            return inverse_rms(
-                p_squares[t], mean_share(p_squares[t], 0, eps, "p%d" % t), "p%d" % t
-            )
+            return inverse_rms(p_squares[t], "p%d" % t)
 
         def first_norm(t, inv_p):
             for n in range(BANKS):
@@ -238,33 +219,51 @@ def tile_recursivemamba130m_pb_kernel(
                     in1=h[t][:, columns(n)], op0=ALU.mult, op1=ALU.add,
                 )
 
-        def sum_v(t):
-            for n in range(BANKS):
-                square_sum(v[t][:, columns(n)], v_squares[t], n)
+        def sum_v(t, n):
+            square_sum(v[t][:, columns(n)], v_squares[t], n)
 
-        def second_norm(t):
-            inv_v = inverse_rms(
-                v_squares[t], mean_share(v_squares[t], 0, eps, "v%d" % t), "v%d" % t
+        def second_scale(t):
+            return inverse_rms(v_squares[t], "v%d" % t)
+
+        def store(t, n):
+            nc.sync.dma_start(
+                out=out_rows[t * P : (t + 1) * P, columns(n)], in_=result[t][:, columns(n)]
             )
+
+        def second_norm(t, inv_v):
             for n in range(BANKS):
                 nc.vector.scalar_tensor_tensor(
                     out=result[t][:, columns(n)], in0=v[t][:, columns(n)], scalar=inv_v[:],
-                    in1=loop_gain[:, columns(n)], op0=ALU.mult, op1=ALU.mult,
+                    in1=loop_row[:, columns(n)], op0=ALU.mult, op1=ALU.mult,
                 )
-                nc.sync.dma_start(
-                    out=out_rows[t * P : (t + 1) * P, columns(n)], in_=result[t][:, columns(n)]
+                store(t, n)
+
+        def gain_v(t):
+            for q in range(PIECES):
+                cols = slice(q * PIECE, (q + 1) * PIECE)
+                nc.gpsimd.tensor_tensor(
+                    out=gained[t][:, cols], in0=v[t][:, cols], in1=loop_row[:, cols], op=ALU.mult
                 )
+
+        def scale_v(t, inv_v):
+            for n in range(BANKS):
+                nc.gpsimd.tensor_scalar(
+                    out=result[t][:, columns(n)], in0=gained[t][:, columns(n)], scalar1=inv_v[:],
+                    scalar2=0.0, op0=ALU.mult, op1=ALU.add,
+                )
+                store(t, n)
 
         pending = []
 
         def convert(unit, copy):
             bank = transpose(unit)
-            if pending:
-                quantise(*pending.pop())
+            if len(pending) == 2:
+                quantise(*pending.pop(0))
             pending.append((unit, empty(bank, copy)))
 
         def flush():
-            quantise(*pending.pop())
+            while pending:
+                quantise(*pending.pop(0))
 
         scopy, vcopy = nc.scalar.copy, nc.vector.tensor_copy
 
@@ -276,50 +275,49 @@ def tile_recursivemamba130m_pb_kernel(
             for s in range(2):
                 convert(y_unit(t, s), copies[s % len(copies)])
 
-        h_pieces = [(t, n) for t in range(L_TILES) for n in range(BANKS)]
-        units = [w_unit(c, g) for c in range(1, CHUNKS) for g in range(PASSES)]
+        step_row = spread(1, vcopy)
+        mixer_row = spread(0, vcopy)
+        loop_row = spread(2, vcopy)
+        units = [w_unit(c, g) for c in range(CHUNKS) for g in range(PASSES)]
         units += [y_unit(t, s) for t in range(1, L_TILES) for s in range(2)]
         convert_y(0, [scopy])
-        for g in range(PASSES):
-            convert(w_unit(0, g), scopy)
-        for n in range(BANKS):
-            spread_step(n)
-        for n in range(BANKS):
-            spread_mixer(n)
-        for n in range(BANKS):
-            spread_loop(n)
         for i, unit in enumerate(units):
-            convert(unit, scopy)
-            if i % 2 == 1 and h_pieces:
-                residual(*h_pieces.pop(0))
+            convert(unit, vcopy if i % 4 == 1 else scopy)
         flush()
+        for t in range(L_TILES):
+            residual(t)
         acc00 = product(0, 0)
         square_p(0, 0, acc00)
         gain(0, 0, acc00)
         acc01 = product(0, 1)
         square_p(0, 1, acc01)
-        inv0 = first_scale(0)
+        inv_p = first_scale(0)
         gain(0, 1, acc01)
         acc10 = product(1, 0)
-        first_norm(0, inv0)
+        first_norm(0, inv_p)
         square_p(1, 0, acc10)
-        sum_v(0)
         gain(1, 0, acc10)
+        sum_v(0, 0)
         acc11 = product(1, 1)
-        second_norm(0)
         square_p(1, 1, acc11)
-        inv1 = first_scale(1)
+        inv_p = first_scale(1)
         gain(1, 1, acc11)
+        sum_v(0, 1)
+        inv_v = second_scale(0)
         acc20 = product(2, 0)
-        first_norm(1, inv1)
+        first_norm(1, inv_p)
         square_p(2, 0, acc20)
         gain(2, 0, acc20)
+        second_norm(0, inv_v)
+        sum_v(1, 0)
         acc21 = product(2, 1)
         square_p(2, 1, acc21)
-        inv2 = first_scale(2)
-        sum_v(1)
+        inv_p = first_scale(2)
         gain(2, 1, acc21)
-        first_norm(2, inv2)
-        second_norm(1)
-        sum_v(2)
-        second_norm(2)
+        sum_v(1, 1)
+        inv_v = second_scale(1)
+        first_norm(2, inv_p)
+        second_norm(1, inv_v)
+        for n in range(BANKS):
+            sum_v(2, n)
+        second_norm(2, second_scale(2))

@@ -54,10 +54,7 @@ def tile_recursivemamba130m_pb_kernel(
 
         vec_in = [consts.tile([P, D // P], BF16, name="vec_in%d" % i) for i in range(3)]
         y_raw = [raw.tile([P, K], BF16, name="y_raw%d" % t) for t in range(L_TILES)]
-        w_raw = [
-            [raw.tile([P, CHUNK_TILES, HALF], BF16, name="w_raw%d_%d" % (c, s)) for s in range(2)]
-            for c in range(CHUNKS)
-        ]
+        w_raw = [raw.tile([P, K], BF16, name="w_raw%d" % i) for i in range(D // P)]
         x_raw = [raw.tile([P, D], BF16, name="x_raw%d" % t) for t in range(L_TILES)]
 
         def load_y(t, pieces):
@@ -67,25 +64,19 @@ def tile_recursivemamba130m_pb_kernel(
         def load_x(t):
             nc.sync.dma_start(out=x_raw[t][:], in_=x_rows[t * P : (t + 1) * P, :])
 
-        def load_w(c):
-            for s in range(2):
-                nc.sync.dma_start(
-                    out=w_raw[c][s][:],
-                    in_=out_proj_w[c * CHUNK : (c + 1) * CHUNK, s * HALF : (s + 1) * HALF].rearrange(
-                        "(i p) k -> p i k", p=P
-                    ),
-                )
+        def load_w(i):
+            nc.sync.dma_start(out=w_raw[i][:], in_=out_proj_w[i * P : (i + 1) * P, :])
 
         whole = [slice(0, K)]
         halves = [slice(0, HALF), slice(HALF, K)]
         for i, vec in enumerate((mixer_norm_w, step_emb, loop_norm_w)):
             nc.sync.dma_start(out=vec_in[i][:], in_=vec.rearrange("(p j) -> p j", p=P))
         load_y(0, halves)
-        for c in range(CHUNKS):
-            load_w(c)
+        for i in range(D // P):
+            load_w(i)
+        load_x(0)
         for t in range(1, L_TILES):
             load_y(t, whole)
-        for t in range(L_TILES):
             load_x(t)
 
         eps = consts.tile([P, 1], F32)
@@ -116,22 +107,29 @@ def tile_recursivemamba130m_pb_kernel(
         y_codes = mx.tile([P, L_TILES, PASSES, P], U32, align_bytes=64)
         y_scales = mx.tile([P, L_TILES, PASSES, P], U8, align_bytes=64)
 
-        def w_unit(c, g):
-            s, first = g // HALF_PASSES, (g % HALF_PASSES) * PASS_WORDS
-            cols = slice(c * CHUNK, (c + 1) * CHUNK)
-            blocks = [(w_raw[c][s][:, i, :].bitcast(F32), first) for i in range(CHUNK_TILES)]
-            return blocks, w_codes[:, g, cols], w_scales[:, g, cols]
+        def half(s):
+            return range(s * HALF_PASSES, (s + 1) * HALF_PASSES)
+
+        def blocks(rows, s):
+            return [(rows.bitcast(F32), g * PASS_WORDS) for g in half(s)]
+
+        def w_unit(i, s):
+            cols = slice(i * P, (i + 1) * P)
+            return (
+                blocks(w_raw[i][:], s),
+                [(w_codes[:, g, cols], w_scales[:, g, cols]) for g in half(s)],
+            )
 
         def y_unit(t, s):
             passes = slice(s * HALF_PASSES, (s + 1) * HALF_PASSES)
-            blocks = [
-                (y_raw[t][:].bitcast(F32), g * PASS_WORDS)
-                for g in range(s * HALF_PASSES, (s + 1) * HALF_PASSES)
-            ]
             return (
-                blocks,
-                y_codes[:, t, passes, :].rearrange("p g r -> p (g r)"),
-                y_scales[:, t, passes, :].rearrange("p g r -> p (g r)"),
+                blocks(y_raw[t][:], s),
+                [
+                    (
+                        y_codes[:, t, passes, :].rearrange("p g r -> p (g r)"),
+                        y_scales[:, t, passes, :].rearrange("p g r -> p (g r)"),
+                    )
+                ],
             )
 
         def transpose(unit):
@@ -149,11 +147,14 @@ def tile_recursivemamba130m_pb_kernel(
             return staged
 
         def quantise(unit, staged):
-            nc.vector.quantize_mx(
-                out=unit[1].bitcast(FP8X4),
-                scales=unit[2],
-                in_=staged[:].rearrange("p i r t -> p (i r t)"),
-            )
+            values = staged[:].rearrange("p i r t -> p (i r t)")
+            width = PACK * unit[1][0][0].shape[1]
+            for i, (codes, scales) in enumerate(unit[1]):
+                nc.vector.quantize_mx(
+                    out=codes.bitcast(FP8X4),
+                    scales=scales,
+                    in_=values[:, i * width : (i + 1) * width],
+                )
 
         h = [keep.tile([P, D], F32, name="h%d" % t) for t in range(L_TILES)]
         gained = [keep.tile([P, D], F32, name="gained%d" % t) for t in range(L_TILES)]
@@ -162,10 +163,10 @@ def tile_recursivemamba130m_pb_kernel(
         p_squares = [stats.tile([P, BANKS], F32, name="p_squares%d" % t) for t in range(L_TILES)]
         v_squares = [stats.tile([P, BANKS], F32, name="v_squares%d" % t) for t in range(L_TILES)]
 
-        def residual(t):
+        def residual(t, engine):
             for q in range(PIECES):
                 cols = slice(q * PIECE, (q + 1) * PIECE)
-                nc.gpsimd.tensor_tensor(
+                engine.tensor_tensor(
                     out=h[t][:, cols], in0=x_raw[t][:, cols], in1=step_row[:, cols], op=ALU.add
                 )
 
@@ -267,52 +268,51 @@ def tile_recursivemamba130m_pb_kernel(
 
         scopy, vcopy = nc.scalar.copy, nc.vector.tensor_copy
 
-        def convert_w(c, copies):
-            for g in range(PASSES):
-                convert(w_unit(c, g), copies[g % len(copies)])
-
-        def convert_y(t, copies):
-            for s in range(2):
-                convert(y_unit(t, s), copies[s % len(copies)])
-
+        w_units = [w_unit(i, s) for i in range(D // P) for s in range(2)]
         step_row = spread(1, vcopy)
+        for s in range(2):
+            convert(y_unit(0, s), scopy)
         mixer_row = spread(0, vcopy)
-        loop_row = spread(2, vcopy)
-        units = [w_unit(c, g) for c in range(CHUNKS) for g in range(PASSES)]
-        units += [y_unit(t, s) for t in range(1, L_TILES) for s in range(2)]
-        convert_y(0, [scopy])
-        for i, unit in enumerate(units):
+        for i, unit in enumerate(w_units):
             convert(unit, vcopy if i % 4 == 1 else scopy)
+            if i == len(w_units) // 2:
+                loop_row = spread(2, vcopy)
         flush()
-        for t in range(L_TILES):
-            residual(t)
         acc00 = product(0, 0)
         square_p(0, 0, acc00)
+        residual(0, nc.vector)
+        residual(1, nc.gpsimd)
+        residual(2, nc.gpsimd)
         gain(0, 0, acc00)
         acc01 = product(0, 1)
         square_p(0, 1, acc01)
         inv_p = first_scale(0)
         gain(0, 1, acc01)
-        acc10 = product(1, 0)
+        convert(y_unit(1, 0), scopy)
+        convert(y_unit(1, 1), scopy)
+        convert(y_unit(2, 0), scopy)
         first_norm(0, inv_p)
-        square_p(1, 0, acc10)
-        gain(1, 0, acc10)
         sum_v(0, 0)
+        convert(y_unit(2, 1), scopy)
+        flush()
+        sum_v(0, 1)
+        inv_v = second_scale(0)
+        acc10 = product(1, 0)
+        square_p(1, 0, acc10)
+        second_norm(0, inv_v)
+        gain(1, 0, acc10)
         acc11 = product(1, 1)
         square_p(1, 1, acc11)
         inv_p = first_scale(1)
         gain(1, 1, acc11)
-        sum_v(0, 1)
-        inv_v = second_scale(0)
         acc20 = product(2, 0)
         first_norm(1, inv_p)
         square_p(2, 0, acc20)
         gain(2, 0, acc20)
-        second_norm(0, inv_v)
-        sum_v(1, 0)
         acc21 = product(2, 1)
         square_p(2, 1, acc21)
         inv_p = first_scale(2)
+        sum_v(1, 0)
         gain(2, 1, acc21)
         sum_v(1, 1)
         inv_v = second_scale(1)

@@ -162,6 +162,8 @@ def tile_recursivemamba130m_pb_kernel(
         result = [keep.tile([P, D], F32, name="result%d" % t) for t in range(L_TILES)]
         p_squares = [stats.tile([P, BANKS], F32, name="p_squares%d" % t) for t in range(L_TILES)]
         v_squares = [stats.tile([P, BANKS], F32, name="v_squares%d" % t) for t in range(L_TILES)]
+        p_share = [stats.tile([P, 1], F32, name="p_share%d" % t) for t in range(L_TILES)]
+        v_share = [stats.tile([P, 1], F32, name="v_share%d" % t) for t in range(L_TILES)]
 
         def residual(t, engine):
             for q in range(PIECES):
@@ -184,26 +186,26 @@ def tile_recursivemamba130m_pb_kernel(
                 )
             return acc
 
-        def inverse_rms(squares, name):
-            share = stats.tile([P, 1], F32, name="share_" + name)
-            nc.scalar.activation(
-                out=share[:], in_=squares[:, 0:1], func=ACT.Identity, scale=1.0 / D, bias=eps[:]
-            )
-            inv = stats.tile([P, 1], F32, name="inv_" + name)
-            nc.scalar.activation(
-                out=inv[:], in_=squares[:, 1:2], func=ACT.Abs_reciprocal_sqrt,
-                scale=1.0 / D, bias=share[:],
-            )
-            return inv
-
-        def square_sum(src, sums, n):
+        def square_sum(src, sums, n, share):
             squares = scrap.tile([P, BANK], BF16, name="squares")
             nc.scalar.activation(
                 out=squares[:], in_=src, func=ACT.Square, accum_out=sums[:, n : n + 1]
             )
+            if n == 0:
+                nc.scalar.activation(
+                    out=share[:], in_=sums[:, 0:1], func=ACT.Identity, scale=1.0 / D, bias=eps[:]
+                )
+
+        def inverse_rms(sums, share, name):
+            inv = stats.tile([P, 1], F32, name="inv_" + name)
+            nc.scalar.activation(
+                out=inv[:], in_=sums[:, 1:2], func=ACT.Abs_reciprocal_sqrt,
+                scale=1.0 / D, bias=share[:],
+            )
+            return inv
 
         def square_p(t, n, acc):
-            square_sum(acc[:], p_squares[t], n)
+            square_sum(acc[:], p_squares[t], n, p_share[t])
 
         def gain(t, n, acc):
             nc.vector.tensor_tensor(
@@ -211,7 +213,7 @@ def tile_recursivemamba130m_pb_kernel(
             )
 
         def first_scale(t):
-            return inverse_rms(p_squares[t], "p%d" % t)
+            return inverse_rms(p_squares[t], p_share[t], "p%d" % t)
 
         def first_norm(t, inv_p):
             for n in range(BANKS):
@@ -221,10 +223,10 @@ def tile_recursivemamba130m_pb_kernel(
                 )
 
         def sum_v(t, n):
-            square_sum(v[t][:, columns(n)], v_squares[t], n)
+            square_sum(v[t][:, columns(n)], v_squares[t], n, v_share[t])
 
         def second_scale(t):
-            return inverse_rms(v_squares[t], "v%d" % t)
+            return inverse_rms(v_squares[t], v_share[t], "v%d" % t)
 
         def store(t, n):
             nc.sync.dma_start(
@@ -290,18 +292,19 @@ def tile_recursivemamba130m_pb_kernel(
         gain(0, 1, acc01)
         convert(y_unit(1, 0), scopy)
         convert(y_unit(1, 1), scopy)
-        convert(y_unit(2, 0), scopy)
-        first_norm(0, inv_p)
-        sum_v(0, 0)
-        convert(y_unit(2, 1), scopy)
         flush()
+        convert(y_unit(2, 0), scopy)
+        convert(y_unit(2, 1), scopy)
+        first_norm(0, inv_p)
+        flush()
+        sum_v(0, 0)
         sum_v(0, 1)
         inv_v = second_scale(0)
         acc10 = product(1, 0)
-        square_p(1, 0, acc10)
-        second_norm(0, inv_v)
         gain(1, 0, acc10)
+        square_p(1, 0, acc10)
         acc11 = product(1, 1)
+        second_norm(0, inv_v)
         square_p(1, 1, acc11)
         inv_p = first_scale(1)
         gain(1, 1, acc11)

@@ -70,7 +70,7 @@ def tile_recursivemamba130m_pb_kernel(
         whole = [slice(0, K)]
         halves = [slice(0, HALF), slice(HALF, K)]
         for i, vec in enumerate((mixer_norm_w, step_emb, loop_norm_w)):
-            nc.sync.dma_start(out=vec_in[i][:], in_=vec.rearrange("(p j) -> p j", p=P))
+            nc.scalar.dma_start(out=vec_in[i][:], in_=vec.rearrange("(p j) -> p j", p=P))
         load_y(0, halves)
         for i in range(D // P):
             load_w(i)
@@ -186,15 +186,16 @@ def tile_recursivemamba130m_pb_kernel(
                 )
             return acc
 
-        def square_sum(src, sums, n, share):
+        def square_sum(src, sums, n):
             squares = scrap.tile([P, BANK], BF16, name="squares")
             nc.scalar.activation(
                 out=squares[:], in_=src, func=ACT.Square, accum_out=sums[:, n : n + 1]
             )
-            if n == 0:
-                nc.scalar.activation(
-                    out=share[:], in_=sums[:, 0:1], func=ACT.Identity, scale=1.0 / D, bias=eps[:]
-                )
+
+        def first_share(sums, share):
+            nc.scalar.activation(
+                out=share[:], in_=sums[:, 0:1], func=ACT.Identity, scale=1.0 / D, bias=eps[:]
+            )
 
         def inverse_rms(sums, share, name):
             inv = stats.tile([P, 1], F32, name="inv_" + name)
@@ -205,7 +206,9 @@ def tile_recursivemamba130m_pb_kernel(
             return inv
 
         def square_p(t, n, acc):
-            square_sum(acc[:], p_squares[t], n, p_share[t])
+            if n == 1:
+                first_share(p_squares[t], p_share[t])
+            square_sum(acc[:], p_squares[t], n)
 
         def gain(t, n, acc):
             nc.vector.tensor_tensor(
@@ -223,9 +226,10 @@ def tile_recursivemamba130m_pb_kernel(
                 )
 
         def sum_v(t, n):
-            square_sum(v[t][:, columns(n)], v_squares[t], n, v_share[t])
+            square_sum(v[t][:, columns(n)], v_squares[t], n)
 
         def second_scale(t):
+            first_share(v_squares[t], v_share[t])
             return inverse_rms(v_squares[t], v_share[t], "v%d" % t)
 
         def store(t, n):

@@ -26,8 +26,6 @@ HALF_PASSES = PASSES // 2
 BANK = 512
 BANKS = D // BANK
 VEC_WORDS = D // 2 // P
-PIECE = 256
-PIECES = D // PIECE
 
 FLOPS = 2 * L * D * K
 
@@ -72,12 +70,19 @@ def tile_recursivemamba130m_pb_kernel(
         for i, vec in enumerate((mixer_norm_w, step_emb, loop_norm_w)):
             nc.scalar.dma_start(out=vec_in[i][:], in_=vec.rearrange("(p j) -> p j", p=P))
         load_y(0, halves)
-        for i in range(D // P):
-            load_w(i)
+        load_w(0)
+        load_w(1)
+        load_w(2)
+        load_w(3)
+        load_w(4)
+        load_w(5)
+        load_w(6)
+        load_w(7)
         load_x(0)
-        for t in range(1, L_TILES):
-            load_y(t, whole)
-            load_x(t)
+        load_y(1, whole)
+        load_x(1)
+        load_y(2, whole)
+        load_x(2)
 
         eps = consts.tile([P, 1], F32)
         nc.vector.memset(eps[:], EPS)
@@ -85,6 +90,8 @@ def tile_recursivemamba130m_pb_kernel(
         nc.scalar.activation(out=warm[:], in_=eps[:], func=ACT.Abs_reciprocal_sqrt)
         ident = consts.tile([P, P], F32)
         make_identity(nc, ident[:])
+        ident_bf = consts.tile([P, P], BF16)
+        make_identity(nc, ident_bf[:])
         def spread(i, copy):
             words = vec_in[i][:].bitcast(F32)
             bank = tr_psum.tile([P, VEC_WORDS, P], F32, name="bank")
@@ -156,7 +163,6 @@ def tile_recursivemamba130m_pb_kernel(
                     in_=values[:, i * width : (i + 1) * width],
                 )
 
-        h = [keep.tile([P, D], F32, name="h%d" % t) for t in range(L_TILES)]
         gained = [keep.tile([P, D], F32, name="gained%d" % t) for t in range(L_TILES)]
         v = [keep.tile([P, D], F32, name="v%d" % t) for t in range(L_TILES)]
         result = [keep.tile([P, D], F32, name="result%d" % t) for t in range(L_TILES)]
@@ -165,12 +171,32 @@ def tile_recursivemamba130m_pb_kernel(
         p_share = [stats.tile([P, 1], F32, name="p_share%d" % t) for t in range(L_TILES)]
         v_share = [stats.tile([P, 1], F32, name="v_share%d" % t) for t in range(L_TILES)]
 
-        def residual(t, engine):
-            for q in range(PIECES):
-                cols = slice(q * PIECE, (q + 1) * PIECE)
-                engine.tensor_tensor(
-                    out=h[t][:, cols], in0=x_raw[t][:, cols], in1=step_row[:, cols], op=ALU.add
+        def residual(t, bank):
+            h = []
+            for n in range(BANKS):
+                acc = bank()
+                nc.tensor.matmul(
+                    acc[:], lhsT=ident_bf[:], rhs=x_raw[t][:, columns(n)], start=True, stop=False
                 )
+                nc.tensor.matmul(
+                    acc[:], lhsT=ident_bf[:], rhs=step_row[:, columns(n)], start=False, stop=True
+                )
+                h.append(acc[:])
+            return h
+
+        def residual_sbuf(t, engine):
+            h = []
+            for n in range(BANKS):
+                part = keep.tile([P, BANK], F32, name="h%d%d" % (t, n))
+                engine.tensor_tensor(
+                    out=part[:], in0=x_raw[t][:, columns(n)], in1=step_row[:, columns(n)], op=ALU.add
+                )
+                h.append(part[:])
+            return h
+
+        def tr_bank():
+            bank = tr_psum.tile([P, BANK], F32, name="bank")
+            return bank
 
         def product(t, n):
             acc = acc_psum.tile([P, BANK], F32, name="acc")
@@ -218,12 +244,11 @@ def tile_recursivemamba130m_pb_kernel(
         def first_scale(t):
             return inverse_rms(p_squares[t], p_share[t], "p%d" % t)
 
-        def first_norm(t, inv_p):
-            for n in range(BANKS):
-                nc.vector.scalar_tensor_tensor(
-                    out=v[t][:, columns(n)], in0=gained[t][:, columns(n)], scalar=inv_p[:],
-                    in1=h[t][:, columns(n)], op0=ALU.mult, op1=ALU.add,
-                )
+        def first_norm(t, inv_p, h, n):
+            nc.vector.scalar_tensor_tensor(
+                out=v[t][:, columns(n)], in0=gained[t][:, columns(n)], scalar=inv_p[:],
+                in1=h[n], op0=ALU.mult, op1=ALU.add,
+            )
 
         def sum_v(t, n):
             square_sum(v[t][:, columns(n)], v_squares[t], n)
@@ -237,28 +262,12 @@ def tile_recursivemamba130m_pb_kernel(
                 out=out_rows[t * P : (t + 1) * P, columns(n)], in_=result[t][:, columns(n)]
             )
 
-        def second_norm(t, inv_v):
-            for n in range(BANKS):
-                nc.vector.scalar_tensor_tensor(
-                    out=result[t][:, columns(n)], in0=v[t][:, columns(n)], scalar=inv_v[:],
-                    in1=loop_row[:, columns(n)], op0=ALU.mult, op1=ALU.mult,
-                )
-                store(t, n)
-
-        def gain_v(t):
-            for q in range(PIECES):
-                cols = slice(q * PIECE, (q + 1) * PIECE)
-                nc.gpsimd.tensor_tensor(
-                    out=gained[t][:, cols], in0=v[t][:, cols], in1=loop_row[:, cols], op=ALU.mult
-                )
-
-        def scale_v(t, inv_v):
-            for n in range(BANKS):
-                nc.gpsimd.tensor_scalar(
-                    out=result[t][:, columns(n)], in0=gained[t][:, columns(n)], scalar1=inv_v[:],
-                    scalar2=0.0, op0=ALU.mult, op1=ALU.add,
-                )
-                store(t, n)
+        def second_norm(t, inv_v, n):
+            nc.vector.scalar_tensor_tensor(
+                out=result[t][:, columns(n)], in0=v[t][:, columns(n)], scalar=inv_v[:],
+                in1=loop_row[:, columns(n)], op0=ALU.mult, op1=ALU.mult,
+            )
+            store(t, n)
 
         pending = []
 
@@ -274,57 +283,76 @@ def tile_recursivemamba130m_pb_kernel(
 
         scopy, vcopy = nc.scalar.copy, nc.vector.tensor_copy
 
-        w_units = [w_unit(i, s) for i in range(D // P) for s in range(2)]
         step_row = spread(1, vcopy)
-        for s in range(2):
-            convert(y_unit(0, s), scopy)
+        convert(y_unit(0, 0), scopy)
+        convert(y_unit(0, 1), scopy)
         mixer_row = spread(0, vcopy)
-        for i, unit in enumerate(w_units):
-            convert(unit, vcopy if i % 4 == 1 else scopy)
-            if i == len(w_units) // 2:
-                loop_row = spread(2, vcopy)
+        convert(w_unit(0, 0), scopy)
+        convert(w_unit(0, 1), vcopy)
+        convert(w_unit(1, 0), scopy)
+        convert(w_unit(1, 1), scopy)
+        convert(w_unit(2, 0), scopy)
+        convert(w_unit(2, 1), vcopy)
+        convert(w_unit(3, 0), scopy)
+        convert(w_unit(3, 1), scopy)
+        convert(w_unit(4, 0), scopy)
+        convert(w_unit(4, 1), vcopy)
+        loop_row = spread(2, vcopy)
+        convert(w_unit(5, 0), scopy)
+        convert(w_unit(5, 1), scopy)
+        convert(w_unit(6, 0), scopy)
+        convert(w_unit(6, 1), vcopy)
+        convert(w_unit(7, 0), scopy)
+        convert(w_unit(7, 1), scopy)
         flush()
         acc00 = product(0, 0)
         square_p(0, 0, acc00)
-        residual(0, nc.vector)
-        residual(1, nc.gpsimd)
-        residual(2, nc.gpsimd)
+        h0 = residual_sbuf(0, nc.vector)
         gain(0, 0, acc00)
         acc01 = product(0, 1)
         square_p(0, 1, acc01)
-        inv_p = first_scale(0)
+        inv_p0 = first_scale(0)
         gain(0, 1, acc01)
         convert(y_unit(1, 0), scopy)
         convert(y_unit(1, 1), scopy)
         flush()
         convert(y_unit(2, 0), scopy)
         convert(y_unit(2, 1), scopy)
-        first_norm(0, inv_p)
+        first_norm(0, inv_p0, h0, 0)
+        first_norm(0, inv_p0, h0, 1)
         flush()
         sum_v(0, 0)
         sum_v(0, 1)
-        inv_v = second_scale(0)
+        inv_v0 = second_scale(0)
+        h1 = residual(1, tr_bank)
         acc10 = product(1, 0)
         gain(1, 0, acc10)
         square_p(1, 0, acc10)
         acc11 = product(1, 1)
-        second_norm(0, inv_v)
+        second_norm(0, inv_v0, 0)
+        second_norm(0, inv_v0, 1)
         square_p(1, 1, acc11)
-        inv_p = first_scale(1)
+        inv_p1 = first_scale(1)
         gain(1, 1, acc11)
+        h2 = residual(2, tr_bank)
         acc20 = product(2, 0)
-        first_norm(1, inv_p)
+        first_norm(1, inv_p1, h1, 0)
+        first_norm(1, inv_p1, h1, 1)
         square_p(2, 0, acc20)
         gain(2, 0, acc20)
         acc21 = product(2, 1)
         square_p(2, 1, acc21)
-        inv_p = first_scale(2)
+        inv_p2 = first_scale(2)
         sum_v(1, 0)
         gain(2, 1, acc21)
         sum_v(1, 1)
-        inv_v = second_scale(1)
-        first_norm(2, inv_p)
-        second_norm(1, inv_v)
-        for n in range(BANKS):
-            sum_v(2, n)
-        second_norm(2, second_scale(2))
+        inv_v1 = second_scale(1)
+        first_norm(2, inv_p2, h2, 0)
+        first_norm(2, inv_p2, h2, 1)
+        second_norm(1, inv_v1, 0)
+        second_norm(1, inv_v1, 1)
+        sum_v(2, 0)
+        sum_v(2, 1)
+        inv_v2 = second_scale(2)
+        second_norm(2, inv_v2, 0)
+        second_norm(2, inv_v2, 1)

@@ -78,10 +78,10 @@ def tile_recursivemamba130m_pb_kernel(
         load_w(5)
         load_w(6)
         load_w(7)
-        load_x(0)
         load_y(1, whole)
-        load_x(1)
+        load_x(0)
         load_y(2, whole)
+        load_x(1)
         load_x(2)
 
         eps = consts.tile([P, 1], F32)
@@ -194,9 +194,27 @@ def tile_recursivemamba130m_pb_kernel(
                 h.append(part[:])
             return h
 
+        def acc_bank():
+            acc = acc_psum.tile([P, BANK], F32, name="acc")
+            return acc
+
         def tr_bank():
             bank = tr_psum.tile([P, BANK], F32, name="bank")
             return bank
+
+        def product_part(acc, t, c):
+            cols = slice(c * CHUNK, (c + 1) * CHUNK)
+            first = (c % 2) * CHUNK
+            for g in range(PASSES):
+                nc.tensor.matmul_mx(
+                    out=acc[:, first : first + CHUNK],
+                    lhsT=y_codes[:, t, g, :].bitcast(FP8X4),
+                    lhsT_scale=y_scales[:, t, g, :],
+                    rhs=w_codes[:, g, cols].bitcast(FP8X4),
+                    rhs_scale=w_scales[:, g, cols],
+                    start=(g == 0),
+                    stop=(g == PASSES - 1),
+                )
 
         def product(t, n):
             acc = acc_psum.tile([P, BANK], F32, name="acc")
@@ -219,8 +237,9 @@ def tile_recursivemamba130m_pb_kernel(
             )
 
         def first_share(sums, share):
-            nc.scalar.activation(
-                out=share[:], in_=sums[:, 0:1], func=ACT.Identity, scale=1.0 / D, bias=eps[:]
+            nc.gpsimd.tensor_scalar(
+                out=share[:], in0=sums[:, 0:1], scalar1=1.0 / D, scalar2=EPS,
+                op0=ALU.mult, op1=ALU.add,
             )
 
         def inverse_rms(sums, share, name):
@@ -232,8 +251,6 @@ def tile_recursivemamba130m_pb_kernel(
             return inv
 
         def square_p(t, n, acc):
-            if n == 1:
-                first_share(p_squares[t], p_share[t])
             square_sum(acc[:], p_squares[t], n)
 
         def gain(t, n, acc):
@@ -253,8 +270,21 @@ def tile_recursivemamba130m_pb_kernel(
         def sum_v(t, n):
             square_sum(v[t][:, columns(n)], v_squares[t], n)
 
+        def sum_v_all(t):
+            squares = scrap.tile([P, D], BF16, name="squares_all")
+            nc.scalar.activation(
+                out=squares[:], in_=v[t][:], func=ACT.Square, accum_out=v_squares[t][:, 0:1]
+            )
+
+        def second_scale_all(t):
+            inv = stats.tile([P, 1], F32, name="inv_all%d" % t)
+            nc.scalar.activation(
+                out=inv[:], in_=v_squares[t][:, 0:1], func=ACT.Abs_reciprocal_sqrt,
+                scale=1.0 / D, bias=eps[:],
+            )
+            return inv
+
         def second_scale(t):
-            first_share(v_squares[t], v_share[t])
             return inverse_rms(v_squares[t], v_share[t], "v%d" % t)
 
         def store(t, n):
@@ -266,6 +296,19 @@ def tile_recursivemamba130m_pb_kernel(
             nc.vector.scalar_tensor_tensor(
                 out=result[t][:, columns(n)], in0=v[t][:, columns(n)], scalar=inv_v[:],
                 in1=loop_row[:, columns(n)], op0=ALU.mult, op1=ALU.mult,
+            )
+            store(t, n)
+
+        def pool_gain(t, n):
+            nc.gpsimd.tensor_tensor(
+                out=gained[t][:, columns(n)], in0=v[t][:, columns(n)],
+                in1=loop_row[:, columns(n)], op=ALU.mult,
+            )
+
+        def pool_norm(t, inv_v, n):
+            nc.gpsimd.tensor_scalar(
+                out=result[t][:, columns(n)], in0=gained[t][:, columns(n)], scalar1=inv_v[:],
+                scalar2=0.0, op0=ALU.mult, op1=ALU.add,
             )
             store(t, n)
 
@@ -304,54 +347,59 @@ def tile_recursivemamba130m_pb_kernel(
         convert(w_unit(6, 1), vcopy)
         convert(w_unit(7, 0), scopy)
         convert(w_unit(7, 1), scopy)
-        flush()
         acc00 = product(0, 0)
         square_p(0, 0, acc00)
-        h0 = residual_sbuf(0, nc.vector)
-        gain(0, 0, acc00)
-        acc01 = product(0, 1)
-        square_p(0, 1, acc01)
-        inv_p0 = first_scale(0)
-        gain(0, 1, acc01)
+        first_share(p_squares[0], p_share[0])
         convert(y_unit(1, 0), scopy)
         convert(y_unit(1, 1), scopy)
+        acc01 = product(0, 1)
+        gain(0, 0, acc00)
+        h0 = residual_sbuf(0, nc.vector)
         flush()
+        square_p(0, 1, acc01)
+        inv_p0 = first_scale(0)
         convert(y_unit(2, 0), scopy)
+        gain(0, 1, acc01)
         convert(y_unit(2, 1), scopy)
         first_norm(0, inv_p0, h0, 0)
         first_norm(0, inv_p0, h0, 1)
         flush()
         sum_v(0, 0)
+        first_share(v_squares[0], v_share[0])
+        acc10 = product(1, 0)
         sum_v(0, 1)
         inv_v0 = second_scale(0)
-        h1 = residual(1, tr_bank)
-        acc10 = product(1, 0)
         gain(1, 0, acc10)
         square_p(1, 0, acc10)
+        first_share(p_squares[1], p_share[1])
         acc11 = product(1, 1)
+        h1 = residual(1, tr_bank)
         second_norm(0, inv_v0, 0)
-        second_norm(0, inv_v0, 1)
         square_p(1, 1, acc11)
         inv_p1 = first_scale(1)
+        second_norm(0, inv_v0, 1)
         gain(1, 1, acc11)
-        h2 = residual(2, tr_bank)
         acc20 = product(2, 0)
         first_norm(1, inv_p1, h1, 0)
         first_norm(1, inv_p1, h1, 1)
         square_p(2, 0, acc20)
+        first_share(p_squares[2], p_share[2])
         gain(2, 0, acc20)
         acc21 = product(2, 1)
+        h2 = residual(2, tr_bank)
         square_p(2, 1, acc21)
         inv_p2 = first_scale(2)
         sum_v(1, 0)
+        first_share(v_squares[1], v_share[1])
         gain(2, 1, acc21)
         sum_v(1, 1)
         inv_v1 = second_scale(1)
         first_norm(2, inv_p2, h2, 0)
         first_norm(2, inv_p2, h2, 1)
         second_norm(1, inv_v1, 0)
-        second_norm(1, inv_v1, 1)
         sum_v(2, 0)
+        first_share(v_squares[2], v_share[2])
+        second_norm(1, inv_v1, 1)
         sum_v(2, 1)
         inv_v2 = second_scale(2)
         second_norm(2, inv_v2, 0)

@@ -19,8 +19,6 @@ PASSES = K // (P * PACK)
 PASS_WORDS = 2 * P
 L_TILES = L // P
 CHUNK = 256
-CHUNK_TILES = CHUNK // P
-CHUNKS = D // CHUNK
 HALF = K // 2
 HALF_PASSES = PASSES // 2
 BANK = 512
@@ -117,20 +115,24 @@ def tile_recursivemamba130m_pb_kernel(
         def half(s):
             return range(s * HALF_PASSES, (s + 1) * HALF_PASSES)
 
-        def blocks(rows, s):
-            return [(rows.bitcast(F32), g * PASS_WORDS) for g in half(s)]
+        in_order = {}
+
+        def blocks(rows, s, name):
+            if name in in_order:
+                return [(in_order[name], g * PASS_WORDS, P, 1) for g in half(s)]
+            return [(rows.bitcast(F32), g * PASS_WORDS, 1, 2) for g in half(s)]
 
         def w_unit(i, s):
             cols = slice(i * P, (i + 1) * P)
             return (
-                blocks(w_raw[i][:], s),
+                blocks(w_raw[i][:], s, "w%d" % i),
                 [(w_codes[:, g, cols], w_scales[:, g, cols]) for g in half(s)],
             )
 
         def y_unit(t, s):
             passes = slice(s * HALF_PASSES, (s + 1) * HALF_PASSES)
             return (
-                blocks(y_raw[t][:], s),
+                blocks(y_raw[t][:], s, "y%d" % t),
                 [
                     (
                         y_codes[:, t, passes, :].rearrange("p g r -> p (g r)"),
@@ -141,10 +143,11 @@ def tile_recursivemamba130m_pb_kernel(
 
         def transpose(unit):
             bank = tr_psum.tile([P, 2, 2, P], F32, name="bank")
-            for i, (words, first) in enumerate(unit[0]):
+            for i, (words, first, offset, step) in enumerate(unit[0]):
                 for u in range(2):
+                    start = first + u * offset
                     nc.tensor.transpose(
-                        bank[:, i, u, :], words[:, first + u : first + PASS_WORDS : 2], ident[:]
+                        bank[:, i, u, :], words[:, start : start + step * (P - 1) + 1 : step], ident[:]
                     )
             return bank
 
@@ -166,7 +169,7 @@ def tile_recursivemamba130m_pb_kernel(
         gained = [keep.tile([P, D], F32, name="gained%d" % t) for t in range(L_TILES)]
         v = [keep.tile([P, D], F32, name="v%d" % t) for t in range(L_TILES)]
         result = [keep.tile([P, D], F32, name="result%d" % t) for t in range(L_TILES)]
-        p_squares = [stats.tile([P, BANKS], F32, name="p_squares%d" % t) for t in range(L_TILES)]
+        p_squares = [stats.tile([P, BANKS + 1], F32, name="p_squares%d" % t) for t in range(L_TILES)]
         v_squares = [stats.tile([P, BANKS], F32, name="v_squares%d" % t) for t in range(L_TILES)]
         p_share = [stats.tile([P, 1], F32, name="p_share%d" % t) for t in range(L_TILES)]
         v_share = [stats.tile([P, 1], F32, name="v_share%d" % t) for t in range(L_TILES)]
@@ -194,27 +197,9 @@ def tile_recursivemamba130m_pb_kernel(
                 h.append(part[:])
             return h
 
-        def acc_bank():
-            acc = acc_psum.tile([P, BANK], F32, name="acc")
-            return acc
-
         def tr_bank():
             bank = tr_psum.tile([P, BANK], F32, name="bank")
             return bank
-
-        def product_part(acc, t, c):
-            cols = slice(c * CHUNK, (c + 1) * CHUNK)
-            first = (c % 2) * CHUNK
-            for g in range(PASSES):
-                nc.tensor.matmul_mx(
-                    out=acc[:, first : first + CHUNK],
-                    lhsT=y_codes[:, t, g, :].bitcast(FP8X4),
-                    lhsT_scale=y_scales[:, t, g, :],
-                    rhs=w_codes[:, g, cols].bitcast(FP8X4),
-                    rhs_scale=w_scales[:, g, cols],
-                    start=(g == 0),
-                    stop=(g == PASSES - 1),
-                )
 
         def product(t, n):
             acc = acc_psum.tile([P, BANK], F32, name="acc")
@@ -270,20 +255,6 @@ def tile_recursivemamba130m_pb_kernel(
         def sum_v(t, n):
             square_sum(v[t][:, columns(n)], v_squares[t], n)
 
-        def sum_v_all(t):
-            squares = scrap.tile([P, D], BF16, name="squares_all")
-            nc.scalar.activation(
-                out=squares[:], in_=v[t][:], func=ACT.Square, accum_out=v_squares[t][:, 0:1]
-            )
-
-        def second_scale_all(t):
-            inv = stats.tile([P, 1], F32, name="inv_all%d" % t)
-            nc.scalar.activation(
-                out=inv[:], in_=v_squares[t][:, 0:1], func=ACT.Abs_reciprocal_sqrt,
-                scale=1.0 / D, bias=eps[:],
-            )
-            return inv
-
         def second_scale(t):
             return inverse_rms(v_squares[t], v_share[t], "v%d" % t)
 
@@ -299,18 +270,13 @@ def tile_recursivemamba130m_pb_kernel(
             )
             store(t, n)
 
-        def pool_gain(t, n):
-            nc.gpsimd.tensor_tensor(
-                out=gained[t][:, columns(n)], in0=v[t][:, columns(n)],
-                in1=loop_row[:, columns(n)], op=ALU.mult,
+        def part_norm(t, inv_v, q):
+            cols = slice(q * CHUNK, (q + 1) * CHUNK)
+            nc.vector.scalar_tensor_tensor(
+                out=result[t][:, cols], in0=v[t][:, cols], scalar=inv_v[:],
+                in1=loop_row[:, cols], op0=ALU.mult, op1=ALU.mult,
             )
-
-        def pool_norm(t, inv_v, n):
-            nc.gpsimd.tensor_scalar(
-                out=result[t][:, columns(n)], in0=gained[t][:, columns(n)], scalar1=inv_v[:],
-                scalar2=0.0, op0=ALU.mult, op1=ALU.add,
-            )
-            store(t, n)
+            nc.sync.dma_start(out=out_rows[t * P : (t + 1) * P, cols], in_=result[t][:, cols])
 
         pending = []
 
@@ -330,6 +296,7 @@ def tile_recursivemamba130m_pb_kernel(
         convert(y_unit(0, 0), scopy)
         convert(y_unit(0, 1), scopy)
         mixer_row = spread(0, vcopy)
+        loop_row = spread(2, scopy)
         convert(w_unit(0, 0), scopy)
         convert(w_unit(0, 1), vcopy)
         convert(w_unit(1, 0), scopy)
@@ -340,11 +307,10 @@ def tile_recursivemamba130m_pb_kernel(
         convert(w_unit(3, 1), scopy)
         convert(w_unit(4, 0), scopy)
         convert(w_unit(4, 1), vcopy)
-        loop_row = spread(2, vcopy)
         convert(w_unit(5, 0), scopy)
         convert(w_unit(5, 1), scopy)
         convert(w_unit(6, 0), scopy)
-        convert(w_unit(6, 1), vcopy)
+        convert(w_unit(6, 1), scopy)
         convert(w_unit(7, 0), scopy)
         convert(w_unit(7, 1), scopy)
         acc00 = product(0, 0)
@@ -353,8 +319,8 @@ def tile_recursivemamba130m_pb_kernel(
         convert(y_unit(1, 0), scopy)
         convert(y_unit(1, 1), scopy)
         acc01 = product(0, 1)
-        gain(0, 0, acc00)
         h0 = residual_sbuf(0, nc.vector)
+        gain(0, 0, acc00)
         flush()
         square_p(0, 1, acc01)
         inv_p0 = first_scale(0)
@@ -403,4 +369,5 @@ def tile_recursivemamba130m_pb_kernel(
         sum_v(2, 1)
         inv_v2 = second_scale(2)
         second_norm(2, inv_v2, 0)
-        second_norm(2, inv_v2, 1)
+        part_norm(2, inv_v2, 2)
+        part_norm(2, inv_v2, 3)

from contextlib import ExitStack

import concourse.mybir as mybir
from concourse.masks import make_identity

F32 = mybir.dt.float32
BF16 = mybir.dt.bfloat16
U32 = mybir.dt.uint32
U8 = mybir.dt.uint8
FP8X4 = mybir.dt.float8_e4m3fn_x4
ACT = mybir.ActivationFunctionType
ALU = mybir.AluOpType

P = 128
L, D, K = 384, 1024, 2048
EPS = 1e-6
PACK = 4
PASSES = K // (P * PACK)
PASS_WORDS = 2 * P
L_TILES = L // P
CHUNK = 256
HALF = K // 2
HALF_PASSES = PASSES // 2
BANK = 512
BANKS = D // BANK
VEC_WORDS = D // 2 // P

FLOPS = 2 * L * D * K


def tile_recursivemamba130m_pb_kernel(
    tc, y, x, step_emb, out_proj_w, mixer_norm_w, loop_norm_w, out
):
    nc = tc.nc
    y_rows = y.flatten_outer_dims()
    x_rows = x.flatten_outer_dims()
    out_rows = out.flatten_outer_dims()

    with ExitStack() as ctx:
        ctx.enter_context(tc.manual_schedule())
        consts = ctx.enter_context(tc.tile_pool(name="consts", bufs=1))
        raw = ctx.enter_context(tc.tile_pool(name="raw", bufs=1))
        mx = ctx.enter_context(tc.tile_pool(name="mx", bufs=1))
        stage = ctx.enter_context(tc.tile_pool(name="stage", bufs=8))
        keep = ctx.enter_context(tc.tile_pool(name="keep", bufs=1))
        scrap = ctx.enter_context(tc.tile_pool(name="scrap", bufs=2))
        stats = ctx.enter_context(tc.tile_pool(name="stats", bufs=1))
        tr_psum = ctx.enter_context(tc.psum_pool(name="tr_psum", bufs=4))
        acc_psum = ctx.enter_context(tc.psum_pool(name="acc_psum", bufs=4))

        vec_in = [consts.tile([P, D // P], BF16, name="vec_in%d" % i) for i in range(3)]
        y_raw = [raw.tile([P, K], BF16, name="y_raw%d" % t) for t in range(L_TILES)]
        w_raw = [raw.tile([P, K], BF16, name="w_raw%d" % i) for i in range(D // P)]
        x_raw = [raw.tile([P, D], BF16, name="x_raw%d" % t) for t in range(L_TILES)]

        def load_y(t, pieces):
            for cols in pieces:
                nc.sync.dma_start(out=y_raw[t][:, cols], in_=y_rows[t * P : (t + 1) * P, cols])

        def load_x(t):
            nc.sync.dma_start(out=x_raw[t][:], in_=x_rows[t * P : (t + 1) * P, :])

        def load_w(i):
            nc.sync.dma_start(out=w_raw[i][:], in_=out_proj_w[i * P : (i + 1) * P, :])

        whole = [slice(0, K)]
        halves = [slice(0, HALF), slice(HALF, K)]
        for i, vec in enumerate((mixer_norm_w, step_emb, loop_norm_w)):
            nc.scalar.dma_start(out=vec_in[i][:], in_=vec.rearrange("(p j) -> p j", p=P))
        load_y(0, halves)
        load_w(0)
        load_w(1)
        load_w(2)
        load_w(3)
        load_w(4)
        load_w(5)
        load_w(6)
        load_w(7)
        load_y(1, whole)
        load_x(0)
        load_y(2, whole)
        load_x(1)
        load_x(2)

        eps = consts.tile([P, 1], F32)
        nc.vector.memset(eps[:], EPS)
        warm = consts.tile([P, 1], F32)
        nc.scalar.activation(out=warm[:], in_=eps[:], func=ACT.Abs_reciprocal_sqrt)
        ident = consts.tile([P, P], F32)
        make_identity(nc, ident[:])
        ident_bf = consts.tile([P, P], BF16)
        make_identity(nc, ident_bf[:])
        def spread(i, copy):
            words = vec_in[i][:].bitcast(F32)
            bank = tr_psum.tile([P, VEC_WORDS, P], F32, name="bank")
            for j in range(VEC_WORDS):
                nc.tensor.transpose(
                    bank[:, j, :], words[:, j : j + 1].to_broadcast([P, P]), ident[:]
                )
            row = consts.tile([P, D], BF16, name="row%d" % i)
            copy(
                out=row[:].bitcast(F32).rearrange("p (w j) -> p w j", j=VEC_WORDS),
                in_=bank[:].rearrange("p j w -> p w j"),
            )
            return row

        def columns(n):
            return slice(n * BANK, (n + 1) * BANK)

        w_codes = mx.tile([P, PASSES, D], U32, align_bytes=64)
        w_scales = mx.tile([P, PASSES, D], U8, align_bytes=64)
        y_codes = mx.tile([P, L_TILES, PASSES, P], U32, align_bytes=64)
        y_scales = mx.tile([P, L_TILES, PASSES, P], U8, align_bytes=64)

        def half(s):
            return range(s * HALF_PASSES, (s + 1) * HALF_PASSES)

        in_order = {}

        def blocks(rows, s, name):
            if name in in_order:
                return [(in_order[name], g * PASS_WORDS, P, 1) for g in half(s)]
            return [(rows.bitcast(F32), g * PASS_WORDS, 1, 2) for g in half(s)]

        def w_unit(i, s):
            cols = slice(i * P, (i + 1) * P)
            return (
                blocks(w_raw[i][:], s, "w%d" % i),
                [(w_codes[:, g, cols], w_scales[:, g, cols]) for g in half(s)],
            )

        def y_unit(t, s):
            passes = slice(s * HALF_PASSES, (s + 1) * HALF_PASSES)
            return (
                blocks(y_raw[t][:], s, "y%d" % t),
                [
                    (
                        y_codes[:, t, passes, :].rearrange("p g r -> p (g r)"),
                        y_scales[:, t, passes, :].rearrange("p g r -> p (g r)"),
                    )
                ],
            )

        def transpose(unit):
            bank = tr_psum.tile([P, 2, 2, P], F32, name="bank")
            for i, (words, first, offset, step) in enumerate(unit[0]):
                for u in range(2):
                    start = first + u * offset
                    nc.tensor.transpose(
                        bank[:, i, u, :], words[:, start : start + step * (P - 1) + 1 : step], ident[:]
                    )
            return bank

        def empty(bank, copy):
            staged = stage.tile([P, 2, P, PACK], BF16, align_bytes=64, name="staged")
            copy(out=staged[:].bitcast(F32), in_=bank[:].rearrange("p i u r -> p i r u"))
            return staged

        def quantise(unit, staged):
            values = staged[:].rearrange("p i r t -> p (i r t)")
            width = PACK * unit[1][0][0].shape[1]
            for i, (codes, scales) in enumerate(unit[1]):
                nc.vector.quantize_mx(
                    out=codes.bitcast(FP8X4),
                    scales=scales,
                    in_=values[:, i * width : (i + 1) * width],
                )

        gained = [keep.tile([P, D], F32, name="gained%d" % t) for t in range(L_TILES)]
        v = [keep.tile([P, D], F32, name="v%d" % t) for t in range(L_TILES)]
        result = [keep.tile([P, D], F32, name="result%d" % t) for t in range(L_TILES)]
        p_squares = [stats.tile([P, BANKS + 1], F32, name="p_squares%d" % t) for t in range(L_TILES)]
        v_squares = [stats.tile([P, BANKS], F32, name="v_squares%d" % t) for t in range(L_TILES)]
        p_share = [stats.tile([P, 1], F32, name="p_share%d" % t) for t in range(L_TILES)]
        v_share = [stats.tile([P, 1], F32, name="v_share%d" % t) for t in range(L_TILES)]

        def residual(t, bank):
            h = []
            for n in range(BANKS):
                acc = bank()
                nc.tensor.matmul(
                    acc[:], lhsT=ident_bf[:], rhs=x_raw[t][:, columns(n)], start=True, stop=False
                )
                nc.tensor.matmul(
                    acc[:], lhsT=ident_bf[:], rhs=step_row[:, columns(n)], start=False, stop=True
                )
                h.append(acc[:])
            return h

        def residual_sbuf(t, engine):
            h = []
            for n in range(BANKS):
                part = keep.tile([P, BANK], F32, name="h%d%d" % (t, n))
                engine.tensor_tensor(
                    out=part[:], in0=x_raw[t][:, columns(n)], in1=step_row[:, columns(n)], op=ALU.add
                )
                h.append(part[:])
            return h

        def tr_bank():
            bank = tr_psum.tile([P, BANK], F32, name="bank")
            return bank

        def product(t, n):
            acc = acc_psum.tile([P, BANK], F32, name="acc")
            for g in range(PASSES):
                nc.tensor.matmul_mx(
                    out=acc[:],
                    lhsT=y_codes[:, t, g, :].bitcast(FP8X4),
                    lhsT_scale=y_scales[:, t, g, :],
                    rhs=w_codes[:, g, columns(n)].bitcast(FP8X4),
                    rhs_scale=w_scales[:, g, columns(n)],
                    start=(g == 0),
                    stop=(g == PASSES - 1),
                )
            return acc

        def square_sum(src, sums, n):
            squares = scrap.tile([P, BANK], BF16, name="squares")
            nc.scalar.activation(
                out=squares[:], in_=src, func=ACT.Square, accum_out=sums[:, n : n + 1]
            )

        def first_share(sums, share):
            nc.gpsimd.tensor_scalar(
                out=share[:], in0=sums[:, 0:1], scalar1=1.0 / D, scalar2=EPS,
                op0=ALU.mult, op1=ALU.add,
            )

        def inverse_rms(sums, share, name):
            inv = stats.tile([P, 1], F32, name="inv_" + name)
            nc.scalar.activation(
                out=inv[:], in_=sums[:, 1:2], func=ACT.Abs_reciprocal_sqrt,
                scale=1.0 / D, bias=share[:],
            )
            return inv

        def square_p(t, n, acc):
            square_sum(acc[:], p_squares[t], n)

        def gain(t, n, acc):
            nc.vector.tensor_tensor(
                out=gained[t][:, columns(n)], in0=acc[:], in1=mixer_row[:, columns(n)], op=ALU.mult
            )

        def first_scale(t):
            return inverse_rms(p_squares[t], p_share[t], "p%d" % t)

        def first_norm(t, inv_p, h, n):
            nc.vector.scalar_tensor_tensor(
                out=v[t][:, columns(n)], in0=gained[t][:, columns(n)], scalar=inv_p[:],
                in1=h[n], op0=ALU.mult, op1=ALU.add,
            )

        def sum_v(t, n):
            square_sum(v[t][:, columns(n)], v_squares[t], n)

        def second_scale(t):
            return inverse_rms(v_squares[t], v_share[t], "v%d" % t)

        def store(t, n):
            nc.sync.dma_start(
                out=out_rows[t * P : (t + 1) * P, columns(n)], in_=result[t][:, columns(n)]
            )

        def second_norm(t, inv_v, n):
            nc.vector.scalar_tensor_tensor(
                out=result[t][:, columns(n)], in0=v[t][:, columns(n)], scalar=inv_v[:],
                in1=loop_row[:, columns(n)], op0=ALU.mult, op1=ALU.mult,
            )
            store(t, n)

        def part_norm(t, inv_v, q):
            cols = slice(q * CHUNK, (q + 1) * CHUNK)
            nc.vector.scalar_tensor_tensor(
                out=result[t][:, cols], in0=v[t][:, cols], scalar=inv_v[:],
                in1=loop_row[:, cols], op0=ALU.mult, op1=ALU.mult,
            )
            nc.sync.dma_start(out=out_rows[t * P : (t + 1) * P, cols], in_=result[t][:, cols])

        pending = []

        def convert(unit, copy):
            bank = transpose(unit)
            if len(pending) == 2:
                quantise(*pending.pop(0))
            pending.append((unit, empty(bank, copy)))

        def flush():
            while pending:
                quantise(*pending.pop(0))

        scopy, vcopy = nc.scalar.copy, nc.vector.tensor_copy

        step_row = spread(1, vcopy)
        convert(y_unit(0, 0), scopy)
        convert(y_unit(0, 1), scopy)
        mixer_row = spread(0, vcopy)
        loop_row = spread(2, scopy)
        convert(w_unit(0, 0), scopy)
        convert(w_unit(0, 1), vcopy)
        convert(w_unit(1, 0), scopy)
        convert(w_unit(1, 1), scopy)
        convert(w_unit(2, 0), scopy)
        convert(w_unit(2, 1), vcopy)
        convert(w_unit(3, 0), scopy)
        convert(w_unit(3, 1), scopy)
        convert(w_unit(4, 0), scopy)
        convert(w_unit(4, 1), vcopy)
        convert(w_unit(5, 0), scopy)
        convert(w_unit(5, 1), scopy)
        convert(w_unit(6, 0), scopy)
        convert(w_unit(6, 1), scopy)
        convert(w_unit(7, 0), scopy)
        convert(w_unit(7, 1), scopy)
        acc00 = product(0, 0)
        square_p(0, 0, acc00)
        first_share(p_squares[0], p_share[0])
        convert(y_unit(1, 0), scopy)
        convert(y_unit(1, 1), scopy)
        acc01 = product(0, 1)
        h0 = residual_sbuf(0, nc.vector)
        gain(0, 0, acc00)
        flush()
        square_p(0, 1, acc01)
        inv_p0 = first_scale(0)
        convert(y_unit(2, 0), scopy)
        gain(0, 1, acc01)
        convert(y_unit(2, 1), scopy)
        first_norm(0, inv_p0, h0, 0)
        first_norm(0, inv_p0, h0, 1)
        flush()
        sum_v(0, 0)
        first_share(v_squares[0], v_share[0])
        acc10 = product(1, 0)
        sum_v(0, 1)
        inv_v0 = second_scale(0)
        gain(1, 0, acc10)
        square_p(1, 0, acc10)
        first_share(p_squares[1], p_share[1])
        acc11 = product(1, 1)
        h1 = residual(1, tr_bank)
        second_norm(0, inv_v0, 0)
        square_p(1, 1, acc11)
        inv_p1 = first_scale(1)
        second_norm(0, inv_v0, 1)
        gain(1, 1, acc11)
        acc20 = product(2, 0)
        first_norm(1, inv_p1, h1, 0)
        first_norm(1, inv_p1, h1, 1)
        square_p(2, 0, acc20)
        first_share(p_squares[2], p_share[2])
        gain(2, 0, acc20)
        acc21 = product(2, 1)
        h2 = residual(2, tr_bank)
        square_p(2, 1, acc21)
        inv_p2 = first_scale(2)
        sum_v(1, 0)
        first_share(v_squares[1], v_share[1])
        gain(2, 1, acc21)
        sum_v(1, 1)
        inv_v1 = second_scale(1)
        first_norm(2, inv_p2, h2, 0)
        first_norm(2, inv_p2, h2, 1)
        second_norm(1, inv_v1, 0)
        sum_v(2, 0)
        first_share(v_squares[2], v_share[2])
        second_norm(1, inv_v1, 1)
        sum_v(2, 1)
        inv_v2 = second_scale(2)
        second_norm(2, inv_v2, 0)
        part_norm(2, inv_v2, 2)
        part_norm(2, inv_v2, 3)
